import numpy as np
import ml_dtypes


def mxq(x, axis, fmt="e4m3"):
    dtype, down = {"e4m3": (ml_dtypes.float8_e4m3fn, 7), "e5m2": (ml_dtypes.float8_e5m2, 14)}[fmt]
    v = np.moveaxis(np.asarray(x, np.float32).astype(ml_dtypes.bfloat16).astype(np.float64), axis, -1)
    blocks = v.reshape(v.shape[:-1] + (-1, 32))
    amax = np.abs(blocks).max(-1, keepdims=True)
    byte = np.maximum(np.where(amax > 0, np.frexp(amax)[1] - 1 + 127, 0) - down, 1)
    scale = np.exp2(byte - 127.0)
    codes = (blocks / scale).astype(np.float32).astype(dtype).astype(np.float64)
    return np.moveaxis((codes * scale).reshape(v.shape), -1, axis)


WIDE = False


def mx_kscale(k):
    if not WIDE:
        return np.ones(k)
    levels = np.array([18, -18])
    if k % 512:
        return np.exp2(np.random.permutation(np.resize(levels, k // 32))).repeat(32)
    a = np.empty((k // 512, 16))
    for p in range(k // 512):
        a[p, :8] = np.random.permutation(np.resize(levels, 8))
        for g in range(8):
            far = levels[np.abs(levels - a[p, g]) >= 10]
            a[p, g + 8] = far[np.random.randint(len(far))]
    return np.exp2(a.ravel()).repeat(32)


BF16 = ml_dtypes.bfloat16


def bf(x):
    return np.asarray(x, np.float32).astype(BF16)


def f64(x):
    return np.asarray(x).astype(np.float64)


D, KW, STRIDE, STACK, B, O = 32, 11, 3, 16, 1024, 512
W_IN = D * D
POS = (D - KW) // STRIDE + 1
K = STACK * POS * POS


def build_mask():
    base_new = np.tile(np.arange(KW), KW)
    addition_new = np.repeat(np.arange(KW) * D, KW)
    index_1 = addition_new + base_new
    index_width = np.tile(index_1, POS)
    addition_width = np.repeat(STRIDE * np.arange(POS), KW * KW)
    index_row = index_width + addition_width
    index_column = np.tile(index_row, POS)
    addition_height = np.repeat(STRIDE * D * np.arange(POS), KW * KW * POS)
    index_final = index_column + addition_height
    stack = np.repeat(np.arange(POS * POS), KW * KW)
    block = np.zeros((POS * POS, W_IN))
    block[stack, index_final] = 1.0
    return np.vstack([block] * STACK)


def setup_inputs():
    s = mx_kscale(B)[:, None]
    u = mx_kscale(O)
    v = mx_kscale(K)
    z0 = bf(np.random.standard_normal((B, W_IN)))
    T3_0 = bf(np.random.standard_normal((K, W_IN)) * 0.7 / np.sqrt(KW * KW))
    mask = bf(build_mask())
    x1 = bf(np.random.standard_normal((B, K)) * 0.7)
    x2 = bf(np.random.standard_normal((B, K)) * 1.4)
    C_w0 = bf(np.random.standard_normal((O, K)) / np.sqrt(K))
    C_b = bf(np.random.standard_normal(O) * 0.5)
    g = bf(np.random.standard_normal((B, O)) * np.exp2(np.random.randint(-6, 1, (B, 1))) * 2.0 / s * u)
    p3 = f64(z0) @ (f64(mask) * f64(T3_0)).T
    return {"z": bf(f64(z0) * s),
            "T3": bf(f64(T3_0) / v[:, None]),
            "mask": mask,
            "x1": x1,
            "x2": x2,
            "C_w": bf(f64(C_w0) * v / u[:, None]),
            "C_b": C_b,
            "p3": np.asarray(p3, np.float32),
            "grad_out": g}


def reference(z, T3, mask, x1, x2, C_w, C_b, p3, grad_out):
    m = f64(mask)
    dx3 = mxq(f64(grad_out), 1, "e5m2") @ mxq(f64(C_w), 0, "e4m3")
    dp3 = 2.0 * f64(x2) * dx3
    dz = mxq(dp3, 1, "e5m2") @ mxq(m * f64(T3), 0, "e4m3")
    dw = mxq(dp3, 0, "e5m2").T @ mxq(f64(z), 0, "e4m3")
    return dz, m * dw

@@ -1,0 +1,392 @@
+from contextlib import ExitStack
+
+import concourse.mybir as mybir
+from concourse.masks import make_identity
+
+F32 = mybir.dt.float32
+BF16 = mybir.dt.bfloat16
+U32 = mybir.dt.uint32
+U8 = mybir.dt.uint8
+E4M3 = mybir.dt.float8_e4m3fn_x4
+E5M2 = mybir.dt.float8_e5m2_x4
+MULT = mybir.AluOpType.mult
+COPY = mybir.ActivationFunctionType.Copy
+
+P = 128
+B, O, K, W = 1024, 512, 1024, 1024
+GROUPS = 2
+T = 4
+SPAN = 640
+WIN2 = 448
+WIN1 = 352
+
+FLOPS = 2 * (B * O * K + 2 * B * K * W)
+BYTES = 2 * (4 * 1024 * 1024 + 2 * 512 * 1024) + 4 * 2 * 1024 * 1024
+
+ORDER = """
+CwA CwB G0 T30 mask x20 T31 z0 x21 CI1A1:V CI0A1:S CI1A0:V CI0A0:V G1 CI0B0:V CI1B1:S CI0B1:V
+CI1B0:V m1 GT01 CQ0 GT00 CQ1 GC01:S ZR1 GC00:S ZR0 MK:S GQ0 MT01:V DX030 DX031 DX021 MT02:G ZR3 M030
+MT00:G M031 DX000 z1 M021 DX020 MT12:G TT03 M020 DX001 TC03:S MT11:G M000 TT02 DX011 M001 TC02:S
+DX010 ZR2 M011 ZI03:S TT00 M010 ZI02:S MT10:G TT01 TC00:S MQ0a TC01:S ZR5 TQ00 AI02:S MQ1 MQ1a ZR7
+AI05:S GT10 ZR4 TQ03 GT11 ZI07:S ZI05:V ZR6 MQ0 GC10:S TQ02 O030 AI01:V AI00:S O031 GC11:V AI06:G
+ZI06:S O020 GQ1 OC030:S ZI00:V DX121 OC020:S TQ01 DX111 OC031:S DX100 M121 ZI01:G O000 AI04:S M111
+ST03 ZI13:G DX120 O010 ZI11:S M100 ZI04:G DX101 M120 ZI14:S DX131 ZI12:G O021 M101 OC000:S TT12
+OC010:V AI03:G OC021:S TT10 M131 ZI15:S ST02 ZI16:G DX130 DX110 TC12:V TC10:S O011 AI07:G M130
+AI14:S O001 AI16:V AI15:S TT13 TQ12 ZI10:V OC011:S O120 ZQ01 OC001:S ST01 O121 TQ10 OC120:S ST00
+TC13:V O100 ZI17:S AQ01 O101 OC121:S TQ13 OC100:S ZQ11 ST12 O130 AI17:S AQ00 O131 OC130:S M110
+OC101:S AQ11 TT11 OC131:S ST10 ZQ00 P7 AI11:S ST13 ZQ10 P6 TC11:S OM7 AI10:G P4 AI12:S OM6 SW7 P5
+TQ11 AI13:S SW6 OM4 O110 OM5 SW4 O111 OC110:S AQ10 SW5 OC111:S P1 ST11 P2 OM1 P0 SW1 OM2 P3 SW2 OM0
+SW0 OM3 SW3
+""".split()
+
+
+def tile_chebyshev_l3_sparsed32_stack_pb_v_kernel(
+    tc, z, T3, mask, x1, x2, C_w, C_b, p3, grad_out, out_0, out_1
+):
+    nc = tc.nc
+    with ExitStack() as ctx:
+        keep = ctx.enter_context(tc.tile_pool(name="keep", bufs=1))
+        stage = ctx.enter_context(tc.tile_pool(name="stage", bufs=4))
+        stage0 = ctx.enter_context(tc.tile_pool(name="stage0", bufs=5))
+        psum_t = ctx.enter_context(tc.psum_pool(name="psum_t", bufs=2))
+        psum_d = ctx.enter_context(tc.psum_pool(name="psum_d", bufs=3))
+        psum_o = ctx.enter_context(tc.psum_pool(name="psum_o", bufs=3))
+
+        cw_raw = [keep.tile([P, T, 512], BF16, name="cw_raw%d" % c) for c in range(2)]
+        g_raw = [keep.tile([P, T, O], BF16, name="g_raw%d" % g) for g in range(GROUPS)]
+        x2_raw = [keep.tile([P, T, K], BF16, name="x2_raw%d" % g) for g in range(GROUPS)]
+        z_raw = [keep.tile([P, T, W], BF16, name="z_raw%d" % g) for g in range(GROUPS)]
+        t3_raw = [keep.tile([P, T, SPAN], BF16, name="t3_raw%d" % h) for h in range(2)]
+        mask_t = keep.tile([P, T, SPAN], BF16, name="mask_t")
+        mask_o = keep.tile([P, WIN1], BF16, name="mask_o")
+        ident = keep.tile([P, P], F32, name="ident")
+        zeros = keep.tile([P, 672], F32, name="zeros")
+
+        cw_il = keep.tile([P, 2, 512, T], BF16, name="cw_il", align_bytes=64)
+        cw_codes = keep.tile([P, 2, 512], U32, name="cw_codes", align_bytes=64)
+        cw_scales = keep.tile([P, 2, 512], U8, name="cw_scales", align_bytes=64)
+        g_il = [keep.tile([P, T, P, 2], F32, name="g_il%d" % g, align_bytes=64) for g in range(GROUPS)]
+        g_codes = [keep.tile([P, T, P], U32, name="g_codes%d" % g, align_bytes=64) for g in range(GROUPS)]
+        g_scales = [keep.tile([P, T, P], U8, name="g_scales%d" % g, align_bytes=64) for g in range(GROUPS)]
+        m_il = [keep.tile([P, SPAN, T], BF16, name="m_il%d" % h, align_bytes=64) for h in range(2)]
+        m_codes = [keep.tile([P, W], U32, name="m_codes%d" % h, align_bytes=64) for h in range(2)]
+        m_scales = [keep.tile([P, W], U8, name="m_scales%d" % h, align_bytes=64) for h in range(2)]
+        dp = [keep.tile([P, T, K], BF16, name="dp%d" % g) for g in range(GROUPS)]
+        dpt_codes = [keep.tile([P, T, 2, P], U32, name="dpt_codes%d" % g, align_bytes=64) for g in range(GROUPS)]
+        dpt_scales = [keep.tile([P, T, 2, P], U8, name="dpt_scales%d" % g, align_bytes=64) for g in range(GROUPS)]
+        dpa_il = [keep.tile([P, K, T], BF16, name="dpa_il%d" % g, align_bytes=64) for g in range(GROUPS)]
+        dpa_codes = [keep.tile([P, K], U32, name="dpa_codes%d" % g, align_bytes=64) for g in range(GROUPS)]
+        dpa_scales = [keep.tile([P, K], U8, name="dpa_scales%d" % g, align_bytes=64) for g in range(GROUPS)]
+        z_il = [keep.tile([P, W, T], BF16, name="z_il%d" % g, align_bytes=64) for g in range(GROUPS)]
+        z_codes = [keep.tile([P, W], U32, name="z_codes%d" % g, align_bytes=64) for g in range(GROUPS)]
+        z_scales = [keep.tile([P, W], U8, name="z_scales%d" % g, align_bytes=64) for g in range(GROUPS)]
+
+        cw_v = C_w.rearrange("(p j) k -> p j k", j=T)
+        g_v = grad_out.rearrange("(g p j) o -> g p j o", g=GROUPS, j=T)
+        x2_v = x2.rearrange("(g p j) k -> g p j k", g=GROUPS, j=T)
+        z_v = z.rearrange("(g p j) w -> g p j w", g=GROUPS, j=T)
+        t3_v = T3.rearrange("(s c r) w -> c s r w", s=16, c=4, r=16)
+        mask_v = mask.rearrange("(s c r) w -> c s r w", s=16, c=4, r=16)
+        mask_i = mask.rearrange("(s i j) w -> i s j w", s=16, i=8, j=8)
+        out0_v = out_0.rearrange("(g p t) w -> g t p w", g=GROUPS, t=T)
+        out1_v = out_1.rearrange("(s i j) w -> i s j w", s=16, i=8, j=8)
+
+        psum = {}
+        sbuf = {}
+
+        def copy(engine, out, in_):
+            if engine == "V":
+                nc.vector.tensor_copy(out=out, in_=in_)
+            elif engine == "S":
+                nc.scalar.copy(out=out, in_=in_)
+            else:
+                nc.gpsimd.tensor_scalar(
+                    out=out, in0=in_, scalar1=1.0, scalar2=0.0, op0=MULT, op1=mybir.AluOpType.add
+                )
+
+        def load_cw(c):
+            nc.sync.dma_start(out=cw_raw[c][:], in_=cw_v[:, :, 512 * c : 512 * (c + 1)])
+
+        def load_t3(h):
+            for u in range(2):
+                col = 192 * (2 * h + u)
+                nc.sync.dma_start(
+                    out=t3_raw[h][:, 2 * u : 2 * u + 2, 192 * u : 192 * u + WIN2],
+                    in_=t3_v[2 * h + u, :, :, col : col + WIN2],
+                )
+
+        def load_mask():
+            nc.sync.dma_start(out=mask_t[:, 0:2, 0:WIN2], in_=mask_v[0, :, :, 0:WIN2])
+
+        def mask_copy(engine):
+            copy(engine, mask_t[:, 2:4, 192:SPAN], mask_t[:, 0:2, 0:WIN2])
+
+        def load_mask_o():
+            nc.sync.dma_start(out=mask_o[:], in_=mask_i[0, :, :, 0:WIN1])
+
+        def store_0(g, t):
+            nc.sync.dma_start(out=out0_v[g, t], in_=sbuf["res0", g, t][:])
+
+        def store_1(i):
+            first = 96 * i
+            nc.sync.dma_start(out=out1_v[i, :, :, first : first + WIN1], in_=sbuf["res1", i][:])
+
+        def zero_1(i):
+            left, right = 96 * i, 672 - 96 * i
+            if left > 0:
+                nc.sync.dma_start(out=out1_v[i, :, :, 0:left], in_=zeros[:, 0:left])
+            if right > 0:
+                nc.sync.dma_start(out=out1_v[i, :, :, left + WIN1 : W], in_=zeros[:, 0:right])
+
+        def g_transpose(g, b):
+            ps = psum_t.tile([P, 2, 2, P], F32, name="tp")
+            for a in range(2):
+                words = g_raw[g][:, 2 * b + a, :].bitcast(F32)
+                for u in range(2):
+                    nc.tensor.transpose(ps[:, a, u, :], words[:, u : O // 2 : 2], ident[:])
+            psum["g", g, b] = ps
+
+        def g_copy(g, b, engine):
+            copy(engine, g_il[g][:, 2 * b : 2 * b + 2], psum["g", g, b][:].rearrange("p a u m -> p a m u"))
+
+        def g_quantize(g):
+            nc.vector.quantize_mx(
+                out=g_codes[g][:].rearrange("p t m -> p (t m)").bitcast(E5M2),
+                scales=g_scales[g][:].rearrange("p t m -> p (t m)"),
+                in_=g_il[g][:].rearrange("p t m u -> p (t m u)").bitcast(BF16),
+            )
+
+        def cw_copy(h, c, u, engine):
+            src = cw_raw[c][:].rearrange("p j (s h u r) -> p h u s r j", s=8, h=2, u=2, r=16)[:, h, u]
+            dst = cw_il[:, h].rearrange("p (u s r) j -> p u s r j", u=2, s=16, r=16)[:, u, 8 * c : 8 * c + 8]
+            if engine == "V":
+                nc.vector.tensor_scalar(out=dst, in0=src, scalar1=2.0, scalar2=None, op0=MULT)
+            else:
+                nc.scalar.activation(out=dst, in_=src, func=COPY, scale=2.0)
+
+        def cw_quantize(h):
+            nc.vector.quantize_mx(
+                out=cw_codes[:, h, :].bitcast(E4M3),
+                scales=cw_scales[:, h, :],
+                in_=cw_il[:, h].rearrange("p n j -> p (n j)"),
+            )
+
+        def dx3(g, t, h):
+            ps = psum_d.tile([P, 512], F32, name="dx")
+            nc.tensor.matmul_mx(
+                out=ps[:],
+                lhsT=g_codes[g][:, t, :].bitcast(E5M2),
+                lhsT_scale=g_scales[g][:, t, :],
+                rhs=cw_codes[:, h, :].bitcast(E4M3),
+                rhs_scale=cw_scales[:, h, :],
+                start=True,
+                stop=True,
+            )
+            psum["dx", g, t, h] = ps
+
+        def dp3(g, t, h):
+            x2_p = x2_raw[g][:, t, :].rearrange("p (s h u r) -> p h u s r", s=16, h=2, u=2, r=16)
+            nc.vector.tensor_tensor(
+                out=dp[g][:, t, 512 * h : 512 * (h + 1)].rearrange("p (u s r) -> p u s r", u=2, r=16),
+                in0=psum["dx", g, t, h][:].rearrange("p (u s r) -> p u s r", u=2, r=16),
+                in1=x2_p[:, h],
+                op=MULT,
+            )
+
+        def dpt_transpose(g, t):
+            ps = psum_t.tile([P, 2, 2, P], F32, name="tp")
+            words = dp[g][:, t, :].bitcast(F32)
+            for h in range(2):
+                for u in range(2):
+                    n = 128 * (2 * h + u)
+                    nc.tensor.transpose(ps[:, h, u, :], words[:, n : n + 128], ident[:])
+            psum["dpt", g, t] = ps
+
+        def dpt_copy(g, t, engine):
+            il = stage.tile([P, 2, P, 2], F32, name="dpt_il", align_bytes=64)
+            copy(engine, il[:], psum["dpt", g, t][:].rearrange("p h u m -> p h m u"))
+            sbuf["dpt", g, t] = il
+
+        def dpt_quantize(g, t):
+            nc.vector.quantize_mx(
+                out=dpt_codes[g][:, t].rearrange("p h m -> p (h m)").bitcast(E5M2),
+                scales=dpt_scales[g][:, t].rearrange("p h m -> p (h m)"),
+                in_=sbuf["dpt", g, t][:].rearrange("p h m u -> p (h m u)").bitcast(BF16),
+            )
+
+        def dpa_copy(g, i, engine):
+            hu, lo = i // 2, i % 2
+            dst = dpa_il[g][:, 128 * i : 128 * (i + 1), :]
+            if engine == "G":
+                src = dp[g][:].rearrange("p t (c s l j) -> p c l s j t", c=4, s=16, l=2, j=8)
+                copy(engine, dst.rearrange("p (s j) t -> p s j t", j=8), src[:, hu, lo])
+            else:
+                src = dp[g][:].rearrange("p t (c s l q i) -> p c l s q t i", c=4, s=16, l=2, q=2, i=4)
+                copy(engine, dst.rearrange("p (s q i) t -> p s q t i", s=16, q=2, i=4), src[:, hu, lo])
+
+        def dpa_quantize(g, h):
+            n = slice(512 * h, 512 * (h + 1))
+            nc.vector.quantize_mx(
+                out=dpa_codes[g][:, n].bitcast(E5M2),
+                scales=dpa_scales[g][:, n],
+                in_=dpa_il[g][:, n, :].rearrange("p n t -> p (n t)"),
+            )
+
+        def m_multiply(h, k, engine):
+            a, b, t0, t1 = ((0, 192, 0, 2), (192, 448, 0, 4), (448, 640, 2, 4))[k]
+            (nc.vector if engine == "V" else nc.gpsimd).tensor_tensor(
+                out=m_il[h][:, a:b, t0:t1].rearrange("p (c i) t -> p c t i", i=4),
+                in0=t3_raw[h][:, t0:t1, a:b].rearrange("p t (c i) -> p c t i", i=4),
+                in1=mask_t[:, t0:t1, a:b].rearrange("p t (c i) -> p c t i", i=4),
+                op=MULT,
+            )
+
+        def m_quantize(h, a, n):
+            col = 384 * h + a
+            nc.vector.quantize_mx(
+                out=m_codes[h][:, col : col + n].bitcast(E4M3),
+                scales=m_scales[h][:, col : col + n],
+                in_=m_il[h][:, a : a + n, :].rearrange("p n t -> p (n t)"),
+            )
+
+        def z_copy(g, b, engine):
+            n = slice(128 * b, 128 * (b + 1))
+            copy(
+                engine,
+                z_il[g][:, n, :].rearrange("p (c i) t -> p c t i", i=4),
+                z_raw[g][:, :, n].rearrange("p t (c i) -> p c t i", i=4),
+            )
+
+        def z_quantize(g, b):
+            n = slice(512 * b, 512 * (b + 1))
+            nc.vector.quantize_mx(
+                out=z_codes[g][:, n].bitcast(E4M3),
+                scales=z_scales[g][:, n],
+                in_=z_il[g][:, n, :].rearrange("p n t -> p (n t)"),
+            )
+
+        def product_0(g, t, w):
+            ps = psum_o.tile([P, 512], F32, name="po")
+            for h in range(2):
+                nc.tensor.matmul_mx(
+                    out=ps[:],
+                    lhsT=dpt_codes[g][:, t, h, :].bitcast(E5M2),
+                    lhsT_scale=dpt_scales[g][:, t, h, :],
+                    rhs=m_codes[h][:, 512 * w : 512 * (w + 1)].bitcast(E4M3),
+                    rhs_scale=m_scales[h][:, 512 * w : 512 * (w + 1)],
+                    start=(h == 0),
+                    stop=(h == 1),
+                )
+            psum["o0", g, t, w] = ps
+
+        def result_0(g, t, w, engine):
+            if ("res0", g, t) not in sbuf:
+                res0 = stage0.tile([P, W], F32, name="res0")
+                sbuf["res0", g, t] = res0
+            copy(engine, sbuf["res0", g, t][:, 512 * w : 512 * (w + 1)], psum["o0", g, t, w][:])
+
+        def window(i):
+            return min(96 * i // 64 * 64, W - 512)
+
+        def product_1(i):
+            base = window(i)
+            ps = psum_o.tile([P, 512], F32, name="po")
+            for g in range(GROUPS):
+                nc.tensor.matmul_mx(
+                    out=ps[:],
+                    lhsT=dpa_codes[g][:, 128 * i : 128 * (i + 1)].bitcast(E5M2),
+                    lhsT_scale=dpa_scales[g][:, 128 * i : 128 * (i + 1)],
+                    rhs=z_codes[g][:, base : base + 512].bitcast(E4M3),
+                    rhs_scale=z_scales[g][:, base : base + 512],
+                    start=(g == 0),
+                    stop=(g == GROUPS - 1),
+                )
+            psum["o1", i] = ps
+
+        def result_1(i):
+            first = 96 * i - window(i)
+            res1 = stage.tile([P, WIN1], F32, name="res1")
+            nc.vector.tensor_tensor(
+                out=res1[:], in0=psum["o1", i][:, first : first + WIN1], in1=mask_o[:], op=MULT
+            )
+            sbuf["res1", i] = res1
+
+        with tc.manual_schedule():
+            make_identity(nc, ident[:])
+            for h in range(2):
+                nc.gpsimd.memset(m_il[h][:].rearrange("p n t -> p (n t)").bitcast(U32), 0)
+            for h, (a, b) in enumerate(((SPAN, W), (0, 384))):
+                nc.gpsimd.memset(m_codes[h][:, a:b], 0)
+                nc.gpsimd.memset(m_scales[h][:, a:b].bitcast(U32), 0)
+            nc.gpsimd.memset(zeros[:], 0.0)
+            for step in ORDER:
+                name = step.split(":")[0]
+                engine = step.split(":")[1] if ":" in step else ""
+                d = [int(x) for x in name if x in "01234567"]
+                if name in ("CwA", "CwB"):
+                    load_cw(0 if name == "CwA" else 1)
+                elif name in ("G0", "G1"):
+                    nc.sync.dma_start(out=g_raw[d[0]][:], in_=g_v[d[0]])
+                elif name in ("x20", "x21"):
+                    nc.sync.dma_start(out=x2_raw[d[1]][:], in_=x2_v[d[1]])
+                elif name in ("z0", "z1"):
+                    nc.sync.dma_start(out=z_raw[d[0]][:], in_=z_v[d[0]])
+                elif name == "mask":
+                    load_mask()
+                elif name in ("T30", "T31"):
+                    load_t3(d[1])
+                elif name == "m1":
+                    load_mask_o()
+                elif name[:2] == "CI":
+                    cw_copy(d[0], {"A": 0, "B": 1}[name[3]], int(name[4]), engine)
+                elif name[:2] == "CQ":
+                    cw_quantize(d[0])
+                elif name[:2] == "GT":
+                    g_transpose(*d)
+                elif name[:2] == "GC":
+                    g_copy(*d, engine)
+                elif name[:2] == "GQ":
+                    g_quantize(*d)
+                elif name[:2] == "DX":
+                    dx3(*d)
+                elif name[:2] == "MT":
+                    m_multiply(*d, engine)
+                elif name == "MK":
+                    mask_copy(engine)
+                elif name[:2] == "MQ":
+                    if name[-1] == "a":
+                        m_quantize(d[0], 0, 512)
+                    else:
+                        m_quantize(d[0], 512, 128)
+                elif name[:2] == "TT":
+                    dpt_transpose(*d)
+                elif name[:2] == "TC":
+                    dpt_copy(*d, engine)
+                elif name[:2] == "TQ":
+                    dpt_quantize(*d)
+                elif name[:2] == "OC":
+                    result_0(*d, engine)
+                elif name[:2] == "OM":
+                    result_1(*d)
+                elif name[:2] == "ST":
+                    store_0(*d)
+                elif name[:2] == "SW":
+                    store_1(*d)
+                elif name[:2] == "ZR":
+                    zero_1(*d)
+                elif name[:2] == "ZI":
+                    z_copy(d[0], d[1], engine)
+                elif name[:2] == "ZQ":
+                    z_quantize(*d)
+                elif name[:2] == "AI":
+                    dpa_copy(d[0], d[1], engine)
+                elif name[:2] == "AQ":
+                    dpa_quantize(*d)
+                elif name[0] == "M":
+                    dp3(*d)
+                elif name[0] == "O":
+                    product_0(*d)
+                elif name[0] == "P":
+                    product_1(*d)
+                else:
+                    raise ValueError(step)

@@ -10,34 +10,21 @@ U8 = mybir.dt.uint8
 E4M3 = mybir.dt.float8_e4m3fn_x4
 E5M2 = mybir.dt.float8_e5m2_x4
 MULT = mybir.AluOpType.mult
+ADD = mybir.AluOpType.add
 COPY = mybir.ActivationFunctionType.Copy
 
 P = 128
 B, O, K, W = 1024, 512, 1024, 1024
 GROUPS = 2
 T = 4
+N = 512
 SPAN = 640
 WIN2 = 448
 WIN1 = 352
+SHIFT = 96
 
 FLOPS = 2 * (B * O * K + 2 * B * K * W)
 BYTES = 2 * (4 * 1024 * 1024 + 2 * 512 * 1024) + 4 * 2 * 1024 * 1024
-
-ORDER = """
-CwA CwB G0 T30 mask x20 T31 z0 x21 CI1A1:V CI0A1:S CI1A0:V CI0A0:V G1 CI0B0:V CI1B1:S CI0B1:V
-CI1B0:V m1 GT01 CQ0 GT00 CQ1 GC01:S ZR1 GC00:S ZR0 MK:S GQ0 MT01:V DX030 DX031 DX021 MT02:G ZR3 M030
-MT00:G M031 DX000 z1 M021 DX020 MT12:G TT03 M020 DX001 TC03:S MT11:G M000 TT02 DX011 M001 TC02:S
-DX010 ZR2 M011 ZI03:S TT00 M010 ZI02:S MT10:G TT01 TC00:S MQ0a TC01:S ZR5 TQ00 AI02:S MQ1 MQ1a ZR7
-AI05:S GT10 ZR4 TQ03 GT11 ZI07:S ZI05:V ZR6 MQ0 GC10:S TQ02 O030 AI01:V AI00:S O031 GC11:V AI06:G
-ZI06:S O020 GQ1 OC030:S ZI00:V DX121 OC020:S TQ01 DX111 OC031:S DX100 M121 ZI01:G O000 AI04:S M111
-ST03 ZI13:G DX120 O010 ZI11:S M100 ZI04:G DX101 M120 ZI14:S DX131 ZI12:G O021 M101 OC000:S TT12
-OC010:V AI03:G OC021:S TT10 M131 ZI15:S ST02 ZI16:G DX130 DX110 TC12:V TC10:S O011 AI07:G M130
-AI14:S O001 AI16:V AI15:S TT13 TQ12 ZI10:V OC011:S O120 ZQ01 OC001:S ST01 O121 TQ10 OC120:S ST00
-TC13:V O100 ZI17:S AQ01 O101 OC121:S TQ13 OC100:S ZQ11 ST12 O130 AI17:S AQ00 O131 OC130:S M110
-OC101:S AQ11 TT11 OC131:S ST10 ZQ00 P7 AI11:S ST13 ZQ10 P6 TC11:S OM7 AI10:G P4 AI12:S OM6 SW7 P5
-TQ11 AI13:S SW6 OM4 O110 OM5 SW4 O111 OC110:S AQ10 SW5 OC111:S P1 ST11 P2 OM1 P0 SW1 OM2 P3 SW2 OM0
-SW0 OM3 SW3
-""".split()
 
 
 def tile_chebyshev_l3_sparsed32_stack_pb_v_kernel(
@@ -48,30 +35,29 @@ def tile_chebyshev_l3_sparsed32_stack_pb_v_kernel(
         keep = ctx.enter_context(tc.tile_pool(name="keep", bufs=1))
         stage = ctx.enter_context(tc.tile_pool(name="stage", bufs=4))
         stage0 = ctx.enter_context(tc.tile_pool(name="stage0", bufs=5))
-        psum_t = ctx.enter_context(tc.psum_pool(name="psum_t", bufs=2))
-        psum_d = ctx.enter_context(tc.psum_pool(name="psum_d", bufs=3))
-        psum_o = ctx.enter_context(tc.psum_pool(name="psum_o", bufs=3))
+        banks = ctx.enter_context(tc.psum_pool(name="banks", bufs=8))
 
-        cw_raw = [keep.tile([P, T, 512], BF16, name="cw_raw%d" % c) for c in range(2)]
-        g_raw = [keep.tile([P, T, O], BF16, name="g_raw%d" % g) for g in range(GROUPS)]
-        x2_raw = [keep.tile([P, T, K], BF16, name="x2_raw%d" % g) for g in range(GROUPS)]
+        cw_raw = keep.tile([P, T, K], BF16, name="cw_raw")
+        g_raw = [[keep.tile([P, 2, O], BF16, name="g_raw%d%d" % (g, b)) for b in range(2)] for g in range(GROUPS)]
+        x2_raw = [[keep.tile([P, 2, K], BF16, name="x2_raw%d%d" % (g, b)) for b in range(2)] for g in range(GROUPS)]
         z_raw = [keep.tile([P, T, W], BF16, name="z_raw%d" % g) for g in range(GROUPS)]
-        t3_raw = [keep.tile([P, T, SPAN], BF16, name="t3_raw%d" % h) for h in range(2)]
-        mask_t = keep.tile([P, T, SPAN], BF16, name="mask_t")
+        U_STEP = 2 * SPAN + 2 * SHIFT
+        t3_raw = [keep.tile([P, 2 * U_STEP], BF16, name="t3_raw%d" % h) for h in range(2)]
+        mask_t = keep.tile([P, 2, WIN2], BF16, name="mask_t")
         mask_o = keep.tile([P, WIN1], BF16, name="mask_o")
         ident = keep.tile([P, P], F32, name="ident")
-        zeros = keep.tile([P, 672], F32, name="zeros")
+        zeros = keep.tile([P, W - WIN1], F32, name="zeros")
 
-        cw_il = keep.tile([P, 2, 512, T], BF16, name="cw_il", align_bytes=64)
-        cw_codes = keep.tile([P, 2, 512], U32, name="cw_codes", align_bytes=64)
-        cw_scales = keep.tile([P, 2, 512], U8, name="cw_scales", align_bytes=64)
-        g_il = [keep.tile([P, T, P, 2], F32, name="g_il%d" % g, align_bytes=64) for g in range(GROUPS)]
+        cw_il = keep.tile([P, 2, N, T], BF16, name="cw_il", align_bytes=64)
+        cw_codes = keep.tile([P, 2, N], U32, name="cw_codes", align_bytes=64)
+        cw_scales = keep.tile([P, 2, N], U8, name="cw_scales", align_bytes=64)
         g_codes = [keep.tile([P, T, P], U32, name="g_codes%d" % g, align_bytes=64) for g in range(GROUPS)]
         g_scales = [keep.tile([P, T, P], U8, name="g_scales%d" % g, align_bytes=64) for g in range(GROUPS)]
         m_il = [keep.tile([P, SPAN, T], BF16, name="m_il%d" % h, align_bytes=64) for h in range(2)]
-        m_codes = [keep.tile([P, W], U32, name="m_codes%d" % h, align_bytes=64) for h in range(2)]
-        m_scales = [keep.tile([P, W], U8, name="m_scales%d" % h, align_bytes=64) for h in range(2)]
-        dp = [keep.tile([P, T, K], BF16, name="dp%d" % g) for g in range(GROUPS)]
+        m_codes = keep.tile([P, SPAN + W], U32, name="m_codes", align_bytes=64)
+        m_scales = keep.tile([P, SPAN + W], U8, name="m_scales", align_bytes=64)
+        dp_flat = [keep.tile([P, T * K], BF16, name="dp%d" % g) for g in range(GROUPS)]
+        dp = [d[:].rearrange("p (t k) -> p t k", t=T) for d in dp_flat]
         dpt_codes = [keep.tile([P, T, 2, P], U32, name="dpt_codes%d" % g, align_bytes=64) for g in range(GROUPS)]
         dpt_scales = [keep.tile([P, T, 2, P], U8, name="dpt_scales%d" % g, align_bytes=64) for g in range(GROUPS)]
         dpa_il = [keep.tile([P, K, T], BF16, name="dpa_il%d" % g, align_bytes=64) for g in range(GROUPS)]
@@ -100,26 +86,37 @@ def tile_chebyshev_l3_sparsed32_stack_pb_v_kernel(
             elif engine == "S":
                 nc.scalar.copy(out=out, in_=in_)
             else:
-                nc.gpsimd.tensor_scalar(
-                    out=out, in0=in_, scalar1=1.0, scalar2=0.0, op0=MULT, op1=mybir.AluOpType.add
-                )
+                nc.gpsimd.tensor_scalar(out=out, in0=in_, scalar1=1.0, scalar2=0.0, op0=MULT, op1=ADD)
 
-        def load_cw(c):
-            nc.sync.dma_start(out=cw_raw[c][:], in_=cw_v[:, :, 512 * c : 512 * (c + 1)])
+        def quantize(codes, scales, values, fmt):
+            nc.vector.quantize_mx(out=codes.bitcast(fmt), scales=scales, in_=values)
+
+        def t3_windows(h):
+            by_u = t3_raw[h][:].rearrange("p (u x) -> p u x", u=2)[:, :, 0 : 2 * SPAN]
+            return by_u.rearrange("p u (e c) -> p u e c", e=2)[:, :, :, 0:WIN2]
+
+        def t3_rows(h):
+            return t3_raw[h][:, 0 : T * SPAN].rearrange("p (t c) -> p t c", t=T)
+
+        def load_cw():
+            nc.sync.dma_start(out=cw_raw[:], in_=cw_v)
+
+        def load_g(g, b):
+            nc.sync.dma_start(out=g_raw[g][b][:], in_=g_v[g, :, 2 * b : 2 * b + 2])
+
+        def load_x2(g, b):
+            nc.sync.dma_start(out=x2_raw[g][b][:], in_=x2_v[g, :, 2 * b : 2 * b + 2])
+
+        def load_z(g):
+            nc.sync.dma_start(out=z_raw[g][:], in_=z_v[g])
 
         def load_t3(h):
             for u in range(2):
-                col = 192 * (2 * h + u)
-                nc.sync.dma_start(
-                    out=t3_raw[h][:, 2 * u : 2 * u + 2, 192 * u : 192 * u + WIN2],
-                    in_=t3_v[2 * h + u, :, :, col : col + WIN2],
-                )
+                col = 2 * SHIFT * (2 * h + u)
+                nc.sync.dma_start(out=t3_windows(h)[:, u], in_=t3_v[2 * h + u, :, :, col : col + WIN2])
 
         def load_mask():
-            nc.sync.dma_start(out=mask_t[:, 0:2, 0:WIN2], in_=mask_v[0, :, :, 0:WIN2])
-
-        def mask_copy(engine):
-            copy(engine, mask_t[:, 2:4, 192:SPAN], mask_t[:, 0:2, 0:WIN2])
+            nc.sync.dma_start(out=mask_t[:], in_=mask_v[0, :, :, 0:WIN2])
 
         def load_mask_o():
             nc.sync.dma_start(out=mask_o[:], in_=mask_i[0, :, :, 0:WIN1])
@@ -128,51 +125,50 @@ def tile_chebyshev_l3_sparsed32_stack_pb_v_kernel(
             nc.sync.dma_start(out=out0_v[g, t], in_=sbuf["res0", g, t][:])
 
         def store_1(i):
-            first = 96 * i
+            first = SHIFT * i
             nc.sync.dma_start(out=out1_v[i, :, :, first : first + WIN1], in_=sbuf["res1", i][:])
 
         def zero_1(i):
-            left, right = 96 * i, 672 - 96 * i
+            left, right = SHIFT * i, W - WIN1 - SHIFT * i
             if left > 0:
                 nc.sync.dma_start(out=out1_v[i, :, :, 0:left], in_=zeros[:, 0:left])
             if right > 0:
                 nc.sync.dma_start(out=out1_v[i, :, :, left + WIN1 : W], in_=zeros[:, 0:right])
 
         def g_transpose(g, b):
-            ps = psum_t.tile([P, 2, 2, P], F32, name="tp")
+            ps = banks.tile([P, 2, 2, P], F32, name="bank")
             for a in range(2):
-                words = g_raw[g][:, 2 * b + a, :].bitcast(F32)
+                words = g_raw[g][b][:, a, :].bitcast(F32)
                 for u in range(2):
                     nc.tensor.transpose(ps[:, a, u, :], words[:, u : O // 2 : 2], ident[:])
             psum["g", g, b] = ps
 
-        def g_copy(g, b, engine):
-            copy(engine, g_il[g][:, 2 * b : 2 * b + 2], psum["g", g, b][:].rearrange("p a u m -> p a m u"))
+        def g_copy(g, b, engine="S"):
+            il = stage.tile([P, 2, P, 2], F32, name="words_il", align_bytes=64, bufs=6)
+            copy(engine, il[:], psum["g", g, b][:].rearrange("p a u m -> p a m u"))
+            sbuf["g", g, b] = il
 
-        def g_quantize(g):
-            nc.vector.quantize_mx(
-                out=g_codes[g][:].rearrange("p t m -> p (t m)").bitcast(E5M2),
-                scales=g_scales[g][:].rearrange("p t m -> p (t m)"),
-                in_=g_il[g][:].rearrange("p t m u -> p (t m u)").bitcast(BF16),
+        def g_quantize(g, b):
+            quantize(
+                g_codes[g][:, 2 * b : 2 * b + 2].rearrange("p t m -> p (t m)"),
+                g_scales[g][:, 2 * b : 2 * b + 2].rearrange("p t m -> p (t m)"),
+                sbuf["g", g, b][:].rearrange("p t m u -> p (t m u)").bitcast(BF16),
+                E5M2,
             )
 
-        def cw_copy(h, c, u, engine):
-            src = cw_raw[c][:].rearrange("p j (s h u r) -> p h u s r j", s=8, h=2, u=2, r=16)[:, h, u]
-            dst = cw_il[:, h].rearrange("p (u s r) j -> p u s r j", u=2, s=16, r=16)[:, u, 8 * c : 8 * c + 8]
+        def cw_copy(h, u, s0, s1, engine):
+            src = cw_raw[:].rearrange("p j (s h u r) -> p h u s r j", s=16, h=2, u=2, r=16)[:, h, u, s0:s1]
+            dst = cw_il[:, h].rearrange("p (u s r) j -> p u s r j", u=2, s=16, r=16)[:, u, s0:s1]
             if engine == "V":
                 nc.vector.tensor_scalar(out=dst, in0=src, scalar1=2.0, scalar2=None, op0=MULT)
             else:
                 nc.scalar.activation(out=dst, in_=src, func=COPY, scale=2.0)
 
         def cw_quantize(h):
-            nc.vector.quantize_mx(
-                out=cw_codes[:, h, :].bitcast(E4M3),
-                scales=cw_scales[:, h, :],
-                in_=cw_il[:, h].rearrange("p n j -> p (n j)"),
-            )
+            quantize(cw_codes[:, h, :], cw_scales[:, h, :], cw_il[:, h].rearrange("p n j -> p (n j)"), E4M3)
 
         def dx3(g, t, h):
-            ps = psum_d.tile([P, 512], F32, name="dx")
+            ps = banks.tile([P, N], F32, name="bank")
             nc.tensor.matmul_mx(
                 out=ps[:],
                 lhsT=g_codes[g][:, t, :].bitcast(E5M2),
@@ -185,208 +181,299 @@ def tile_chebyshev_l3_sparsed32_stack_pb_v_kernel(
             psum["dx", g, t, h] = ps
 
         def dp3(g, t, h):
-            x2_p = x2_raw[g][:, t, :].rearrange("p (s h u r) -> p h u s r", s=16, h=2, u=2, r=16)
+            x2_p = x2_raw[g][t // 2][:, t % 2, :].rearrange("p (s h u r) -> p h u s r", s=16, h=2, u=2, r=16)
             nc.vector.tensor_tensor(
-                out=dp[g][:, t, 512 * h : 512 * (h + 1)].rearrange("p (u s r) -> p u s r", u=2, r=16),
+                out=dp[g][:, t, N * h : N * (h + 1)].rearrange("p (u s r) -> p u s r", u=2, r=16),
                 in0=psum["dx", g, t, h][:].rearrange("p (u s r) -> p u s r", u=2, r=16),
                 in1=x2_p[:, h],
                 op=MULT,
             )
 
         def dpt_transpose(g, t):
-            ps = psum_t.tile([P, 2, 2, P], F32, name="tp")
-            words = dp[g][:, t, :].bitcast(F32)
+            ps = banks.tile([P, 2, 2, P], F32, name="bank")
+            words = dp_flat[g][:, K * t : K * (t + 1)].bitcast(F32)
             for h in range(2):
                 for u in range(2):
-                    n = 128 * (2 * h + u)
-                    nc.tensor.transpose(ps[:, h, u, :], words[:, n : n + 128], ident[:])
+                    n = P * (2 * h + u)
+                    nc.tensor.transpose(ps[:, h, u, :], words[:, n : n + P], ident[:])
             psum["dpt", g, t] = ps
 
-        def dpt_copy(g, t, engine):
-            il = stage.tile([P, 2, P, 2], F32, name="dpt_il", align_bytes=64)
+        def dpt_copy(g, t, engine="S"):
+            il = stage.tile([P, 2, P, 2], F32, name="words_il", align_bytes=64, bufs=6)
             copy(engine, il[:], psum["dpt", g, t][:].rearrange("p h u m -> p h m u"))
             sbuf["dpt", g, t] = il
 
         def dpt_quantize(g, t):
-            nc.vector.quantize_mx(
-                out=dpt_codes[g][:, t].rearrange("p h m -> p (h m)").bitcast(E5M2),
-                scales=dpt_scales[g][:, t].rearrange("p h m -> p (h m)"),
-                in_=sbuf["dpt", g, t][:].rearrange("p h m u -> p (h m u)").bitcast(BF16),
+            quantize(
+                dpt_codes[g][:, t].rearrange("p h m -> p (h m)"),
+                dpt_scales[g][:, t].rearrange("p h m -> p (h m)"),
+                sbuf["dpt", g, t][:].rearrange("p h m u -> p (h m u)").bitcast(BF16),
+                E5M2,
             )
 
-        def dpa_copy(g, i, engine):
-            hu, lo = i // 2, i % 2
-            dst = dpa_il[g][:, 128 * i : 128 * (i + 1), :]
+        def dpa_copy(g, c, engine):
+            src = dp[g][:, :, 256 * c : 256 * (c + 1)]
+            dst = dpa_il[g][:, 256 * c : 256 * (c + 1), :]
             if engine == "G":
-                src = dp[g][:].rearrange("p t (c s l j) -> p c l s j t", c=4, s=16, l=2, j=8)
-                copy(engine, dst.rearrange("p (s j) t -> p s j t", j=8), src[:, hu, lo])
+                copy(
+                    engine,
+                    dst.rearrange("p (l s j) t -> p s l j t", l=2, j=8),
+                    src.rearrange("p t (s l j) -> p s l j t", l=2, j=8),
+                )
             else:
-                src = dp[g][:].rearrange("p t (c s l q i) -> p c l s q t i", c=4, s=16, l=2, q=2, i=4)
-                copy(engine, dst.rearrange("p (s q i) t -> p s q t i", s=16, q=2, i=4), src[:, hu, lo])
+                for l in range(2):
+                    copy(
+                        engine,
+                        dst.rearrange("p (l s q i) t -> p l s q t i", l=2, q=2, i=4)[:, l],
+                        src.rearrange("p t (s l q i) -> p l s q t i", l=2, q=2, i=4)[:, l],
+                    )
 
         def dpa_quantize(g, h):
-            n = slice(512 * h, 512 * (h + 1))
-            nc.vector.quantize_mx(
-                out=dpa_codes[g][:, n].bitcast(E5M2),
-                scales=dpa_scales[g][:, n],
-                in_=dpa_il[g][:, n, :].rearrange("p n t -> p (n t)"),
-            )
+            n = slice(N * h, N * (h + 1))
+            quantize(dpa_codes[g][:, n], dpa_scales[g][:, n], dpa_il[g][:, n, :].rearrange("p n t -> p (n t)"), E5M2)
 
-        def m_multiply(h, k, engine):
-            a, b, t0, t1 = ((0, 192, 0, 2), (192, 448, 0, 4), (448, 640, 2, 4))[k]
-            (nc.vector if engine == "V" else nc.gpsimd).tensor_tensor(
-                out=m_il[h][:, a:b, t0:t1].rearrange("p (c i) t -> p c t i", i=4),
-                in0=t3_raw[h][:, t0:t1, a:b].rearrange("p t (c i) -> p c t i", i=4),
-                in1=mask_t[:, t0:t1, a:b].rearrange("p t (c i) -> p c t i", i=4),
+        def interleave(engine, il, rows):
+            copy(engine, il.rearrange("p (c i) t -> p c t i", i=4), rows.rearrange("p t (c i) -> p c t i", i=4))
+
+        def m_multiply(h):
+            nc.vector.tensor_tensor(
+                out=t3_windows(h),
+                in0=t3_windows(h),
+                in1=mask_t[:].unsqueeze(1).to_broadcast([P, 2, 2, WIN2]),
                 op=MULT,
             )
 
-        def m_quantize(h, a, n):
-            col = 384 * h + a
-            nc.vector.quantize_mx(
-                out=m_codes[h][:, col : col + n].bitcast(E4M3),
-                scales=m_scales[h][:, col : col + n],
-                in_=m_il[h][:, a : a + n, :].rearrange("p n t -> p (n t)"),
-            )
+        def m_copy(h, a, b, engine):
+            interleave(engine, m_il[h][:, a:b, :], t3_rows(h)[:, :, a:b])
 
-        def z_copy(g, b, engine):
-            n = slice(128 * b, 128 * (b + 1))
-            copy(
-                engine,
-                z_il[g][:, n, :].rearrange("p (c i) t -> p c t i", i=4),
-                z_raw[g][:, :, n].rearrange("p t (c i) -> p c t i", i=4),
-            )
+        def m_quantize(h):
+            for a, n in ((0, N), (N, SPAN - N)):
+                col = W * h + a
+                quantize(
+                    m_codes[:, col : col + n],
+                    m_scales[:, col : col + n],
+                    m_il[h][:, a : a + n, :].rearrange("p n t -> p (n t)"),
+                    E4M3,
+                )
+
+        def z_copy(g, a, b, engine):
+            interleave(engine, z_il[g][:, a:b, :], z_raw[g][:, :, a:b])
 
         def z_quantize(g, b):
-            n = slice(512 * b, 512 * (b + 1))
-            nc.vector.quantize_mx(
-                out=z_codes[g][:, n].bitcast(E4M3),
-                scales=z_scales[g][:, n],
-                in_=z_il[g][:, n, :].rearrange("p n t -> p (n t)"),
-            )
+            n = slice(N * b, N * (b + 1))
+            quantize(z_codes[g][:, n], z_scales[g][:, n], z_il[g][:, n, :].rearrange("p n t -> p (n t)"), E4M3)
 
         def product_0(g, t, w):
-            ps = psum_o.tile([P, 512], F32, name="po")
+            ps = banks.tile([P, N], F32, name="bank")
             for h in range(2):
+                n = slice(SPAN * h + N * w, SPAN * h + N * (w + 1))
                 nc.tensor.matmul_mx(
                     out=ps[:],
                     lhsT=dpt_codes[g][:, t, h, :].bitcast(E5M2),
                     lhsT_scale=dpt_scales[g][:, t, h, :],
-                    rhs=m_codes[h][:, 512 * w : 512 * (w + 1)].bitcast(E4M3),
-                    rhs_scale=m_scales[h][:, 512 * w : 512 * (w + 1)],
+                    rhs=m_codes[:, n].bitcast(E4M3),
+                    rhs_scale=m_scales[:, n],
                     start=(h == 0),
                     stop=(h == 1),
                 )
             psum["o0", g, t, w] = ps
 
-        def result_0(g, t, w, engine):
+        def result_0(g, t, w, engine="S"):
             if ("res0", g, t) not in sbuf:
-                res0 = stage0.tile([P, W], F32, name="res0")
-                sbuf["res0", g, t] = res0
-            copy(engine, sbuf["res0", g, t][:, 512 * w : 512 * (w + 1)], psum["o0", g, t, w][:])
+                sbuf["res0", g, t] = stage0.tile([P, W], F32, name="res0")
+            copy(engine, sbuf["res0", g, t][:, N * w : N * (w + 1)], psum["o0", g, t, w][:])
 
         def window(i):
-            return min(96 * i // 64 * 64, W - 512)
+            first = SHIFT * i
+            if first + WIN1 <= N or first >= N:
+                return first // N * N
+            return first // 64 * 64
 
         def product_1(i):
             base = window(i)
-            ps = psum_o.tile([P, 512], F32, name="po")
+            ps = banks.tile([P, N], F32, name="bank")
             for g in range(GROUPS):
                 nc.tensor.matmul_mx(
                     out=ps[:],
-                    lhsT=dpa_codes[g][:, 128 * i : 128 * (i + 1)].bitcast(E5M2),
-                    lhsT_scale=dpa_scales[g][:, 128 * i : 128 * (i + 1)],
-                    rhs=z_codes[g][:, base : base + 512].bitcast(E4M3),
-                    rhs_scale=z_scales[g][:, base : base + 512],
+                    lhsT=dpa_codes[g][:, P * i : P * (i + 1)].bitcast(E5M2),
+                    lhsT_scale=dpa_scales[g][:, P * i : P * (i + 1)],
+                    rhs=z_codes[g][:, base : base + N].bitcast(E4M3),
+                    rhs_scale=z_scales[g][:, base : base + N],
                     start=(g == 0),
                     stop=(g == GROUPS - 1),
                 )
             psum["o1", i] = ps
 
         def result_1(i):
-            first = 96 * i - window(i)
-            res1 = stage.tile([P, WIN1], F32, name="res1")
-            nc.vector.tensor_tensor(
-                out=res1[:], in0=psum["o1", i][:, first : first + WIN1], in1=mask_o[:], op=MULT
-            )
+            first = SHIFT * i - window(i)
+            res1 = stage.tile([P, WIN1], F32, name="res1", bufs=8)
+            nc.vector.tensor_tensor(out=res1[:], in0=psum["o1", i][:, first : first + WIN1], in1=mask_o[:], op=MULT)
             sbuf["res1", i] = res1
 
-        with tc.manual_schedule():
-            make_identity(nc, ident[:])
+        def out_0_tile(g, t, engines="SS"):
+            for w in range(2):
+                product_0(g, t, w)
+                result_0(g, t, w, engines[w])
+            store_0(g, t)
+
+        def out_1_tile(i):
+            product_1(i)
+            result_1(i)
+            store_1(i)
+
+        def fill_zeros():
             for h in range(2):
-                nc.gpsimd.memset(m_il[h][:].rearrange("p n t -> p (n t)").bitcast(U32), 0)
-            for h, (a, b) in enumerate(((SPAN, W), (0, 384))):
-                nc.gpsimd.memset(m_codes[h][:, a:b], 0)
-                nc.gpsimd.memset(m_scales[h][:, a:b].bitcast(U32), 0)
-            nc.gpsimd.memset(zeros[:], 0.0)
-            for step in ORDER:
-                name = step.split(":")[0]
-                engine = step.split(":")[1] if ":" in step else ""
-                d = [int(x) for x in name if x in "01234567"]
-                if name in ("CwA", "CwB"):
-                    load_cw(0 if name == "CwA" else 1)
-                elif name in ("G0", "G1"):
-                    nc.sync.dma_start(out=g_raw[d[0]][:], in_=g_v[d[0]])
-                elif name in ("x20", "x21"):
-                    nc.sync.dma_start(out=x2_raw[d[1]][:], in_=x2_v[d[1]])
-                elif name in ("z0", "z1"):
-                    nc.sync.dma_start(out=z_raw[d[0]][:], in_=z_v[d[0]])
-                elif name == "mask":
-                    load_mask()
-                elif name in ("T30", "T31"):
-                    load_t3(d[1])
-                elif name == "m1":
-                    load_mask_o()
-                elif name[:2] == "CI":
-                    cw_copy(d[0], {"A": 0, "B": 1}[name[3]], int(name[4]), engine)
-                elif name[:2] == "CQ":
-                    cw_quantize(d[0])
-                elif name[:2] == "GT":
-                    g_transpose(*d)
-                elif name[:2] == "GC":
-                    g_copy(*d, engine)
-                elif name[:2] == "GQ":
-                    g_quantize(*d)
-                elif name[:2] == "DX":
-                    dx3(*d)
-                elif name[:2] == "MT":
-                    m_multiply(*d, engine)
-                elif name == "MK":
-                    mask_copy(engine)
-                elif name[:2] == "MQ":
-                    if name[-1] == "a":
-                        m_quantize(d[0], 0, 512)
-                    else:
-                        m_quantize(d[0], 512, 128)
-                elif name[:2] == "TT":
-                    dpt_transpose(*d)
-                elif name[:2] == "TC":
-                    dpt_copy(*d, engine)
-                elif name[:2] == "TQ":
-                    dpt_quantize(*d)
-                elif name[:2] == "OC":
-                    result_0(*d, engine)
-                elif name[:2] == "OM":
-                    result_1(*d)
-                elif name[:2] == "ST":
-                    store_0(*d)
-                elif name[:2] == "SW":
-                    store_1(*d)
-                elif name[:2] == "ZR":
-                    zero_1(*d)
-                elif name[:2] == "ZI":
-                    z_copy(d[0], d[1], engine)
-                elif name[:2] == "ZQ":
-                    z_quantize(*d)
-                elif name[:2] == "AI":
-                    dpa_copy(d[0], d[1], engine)
-                elif name[:2] == "AQ":
-                    dpa_quantize(*d)
-                elif name[0] == "M":
-                    dp3(*d)
-                elif name[0] == "O":
-                    product_0(*d)
-                elif name[0] == "P":
-                    product_1(*d)
-                else:
-                    raise ValueError(step)
+                rows = t3_rows(h)
+                nc.vector.memset(rows[:, 0:2, WIN2:SPAN], 0.0)
+                nc.vector.memset(rows[:, 2:4, 0 : SPAN - WIN2], 0.0)
+            nc.vector.memset(m_codes[:, SPAN:W], 0)
+            nc.vector.memset(m_scales[:, SPAN:W].bitcast(U32), 0)
+            nc.vector.memset(zeros[:], 0.0)
+
+        with tc.manual_schedule():
+
+            def dx_dp(g, t, h):
+                dx3(g, t, h)
+                dp3(g, t, h)
+
+            def turn(g, t):
+                dpt_transpose(g, t)
+                dpt_copy(g, t)
+
+            def g_turn(g, b):
+                g_transpose(g, b)
+                g_copy(g, b)
+
+            def products_0(g, t):
+                for w in range(2):
+                    product_0(g, t, w)
+
+            def results_0(g, t, engines="SS"):
+                for w in range(2):
+                    result_0(g, t, w, engines[w])
+                store_0(g, t)
+
+            def finish_1(i):
+                result_1(i)
+                store_1(i)
+
+            make_identity(nc, ident[:])
+            fill_zeros()
+            load_g(0, 0)
+            load_cw()
+            load_g(0, 1)
+            load_mask()
+            load_t3(0)
+            load_x2(0, 0)
+            load_t3(1)
+            load_x2(0, 1)
+            load_g(1, 0)
+            load_g(1, 1)
+            load_z(0)
+            load_x2(1, 0)
+            load_x2(1, 1)
+            load_z(1)
+            load_mask_o()
+
+            g_turn(0, 0)
+            cw_copy(0, 0, 0, 16, "V")
+            cw_copy(0, 1, 0, 5, "V")
+            cw_copy(0, 1, 5, 16, "S")
+            g_quantize(0, 0)
+            cw_copy(1, 0, 0, 8, "V")
+            cw_quantize(0)
+            cw_copy(1, 0, 8, 16, "S")
+            g_turn(0, 1)
+            cw_copy(1, 1, 0, 16, "S")
+            m_multiply(0)
+            m_copy(0, 0, 192, "G")
+            m_copy(0, 192, SPAN, "S")
+            g_quantize(0, 1)
+            dx_dp(0, 0, 0)
+            dx_dp(0, 1, 0)
+            cw_quantize(1)
+            m_multiply(1)
+            m_copy(1, 0, 256, "G")
+            m_copy(1, 256, SPAN, "S")
+            dx_dp(0, 2, 0)
+            dx_dp(0, 3, 0)
+            dpa_copy(0, 0, "G")
+            for t in range(T):
+                dx3(0, t, 1)
+            g_turn(1, 0)
+            g_turn(1, 1)
+            for t in range(T):
+                dp3(0, t, 1)
+            for t in range(T):
+                turn(0, t)
+
+            g_quantize(1, 0)
+            m_quantize(0)
+            m_quantize(1)
+            dpt_quantize(0, 0)
+            g_quantize(1, 1)
+            for t in range(1, T):
+                dpt_quantize(0, t)
+            for c in (2, 3, 1):
+                dpa_copy(0, c, "G")
+            for i in range(5):
+                zero_1(i)
+            for t in range(2):
+                for h in range(2):
+                    dx3(1, t, h)
+            z_copy(0, 0, 512, "S")
+            products_0(0, 0)
+            results_0(0, 0)
+            zero_1(5)
+            for t in range(2):
+                for h in range(2):
+                    dp3(1, t, h)
+            for t in range(2, 4):
+                for h in range(2):
+                    dx3(1, t, h)
+            z_copy(0, 512, 768, "S")
+            turn(1, 0)
+            turn(1, 1)
+            products_0(0, 1)
+            results_0(0, 1)
+            zero_1(6)
+            zero_1(7)
+            for t in range(2, 4):
+                for h in range(2):
+                    dp3(1, t, h)
+            z_copy(0, 768, 1024, "S")
+            turn(1, 2)
+            turn(1, 3)
+            products_0(0, 2)
+            results_0(0, 2)
+            z_copy(1, 0, 512, "V")
+            dpt_quantize(1, 0)
+            dpt_quantize(1, 1)
+            z_quantize(0, 0)
+            for c in range(2):
+                dpa_copy(1, c, "V")
+            dpt_quantize(1, 2)
+            dpt_quantize(1, 3)
+            products_0(0, 3)
+            results_0(0, 3)
+            z_quantize(1, 0)
+            dpa_quantize(0, 0)
+            z_copy(1, 512, 1024, "V")
+            dpa_quantize(1, 0)
+            z_quantize(0, 1)
+            z_quantize(1, 1)
+            for t in range(3):
+                products_0(1, t)
+                results_0(1, t)
+            for c in range(2, 4):
+                dpa_copy(1, c, "V")
+            dpa_quantize(0, 1)
+            dpa_quantize(1, 1)
+            for i in range(2):
+                product_1(i)
+            products_0(1, 3)
+            results_0(1, 3)
+            finish_1(0)
+            finish_1(1)
+            for i in range(2, 8):
+                out_1_tile(i)

@@ -35,7 +35,7 @@ def tile_chebyshev_l3_sparsed32_stack_pb_v_kernel(
         keep = ctx.enter_context(tc.tile_pool(name="keep", bufs=1))
         stage = ctx.enter_context(tc.tile_pool(name="stage", bufs=4))
         stage0 = ctx.enter_context(tc.tile_pool(name="stage0", bufs=5))
-        banks = ctx.enter_context(tc.psum_pool(name="banks", bufs=8))
+        banks = ctx.enter_context(tc.psum_pool(name="banks", bufs=1))
 
         cw_raw = keep.tile([P, T, K], BF16, name="cw_raw")
         g_raw = [[keep.tile([P, 2, O], BF16, name="g_raw%d%d" % (g, b)) for b in range(2)] for g in range(GROUPS)]
@@ -78,6 +78,12 @@ def tile_chebyshev_l3_sparsed32_stack_pb_v_kernel(
         out1_v = out_1.rearrange("(s i j) w -> i s j w", s=16, i=8, j=8)
 
         psum = {}
+        taken = []
+
+        def next_bank():
+            taken.append(banks.tile([P, N], F32, name="bank%d" % (len(taken) % 8)))
+            return taken[-1][:]
+
         sbuf = {}
 
         def copy(engine, out, in_):
@@ -128,15 +134,18 @@ def tile_chebyshev_l3_sparsed32_stack_pb_v_kernel(
             first = SHIFT * i
             nc.sync.dma_start(out=out1_v[i, :, :, first : first + WIN1], in_=sbuf["res1", i][:])
 
+        def zero_rows(width):
+            return zeros[32:96, 0:width].unsqueeze(1).to_broadcast([64, 2, width])
+
         def zero_1(i):
             left, right = SHIFT * i, W - WIN1 - SHIFT * i
             if left > 0:
-                nc.sync.dma_start(out=out1_v[i, :, :, 0:left], in_=zeros[:, 0:left])
+                nc.sync.dma_start(out=out1_v[i, :, :, 0:left], in_=zero_rows(left))
             if right > 0:
-                nc.sync.dma_start(out=out1_v[i, :, :, left + WIN1 : W], in_=zeros[:, 0:right])
+                nc.sync.dma_start(out=out1_v[i, :, :, left + WIN1 : W], in_=zero_rows(right))
 
         def g_transpose(g, b):
-            ps = banks.tile([P, 2, 2, P], F32, name="bank")
+            ps = next_bank().rearrange("p (a u m) -> p a u m", a=2, u=2)
             for a in range(2):
                 words = g_raw[g][b][:, a, :].bitcast(F32)
                 for u in range(2):
@@ -168,7 +177,7 @@ def tile_chebyshev_l3_sparsed32_stack_pb_v_kernel(
             quantize(cw_codes[:, h, :], cw_scales[:, h, :], cw_il[:, h].rearrange("p n j -> p (n j)"), E4M3)
 
         def dx3(g, t, h):
-            ps = banks.tile([P, N], F32, name="bank")
+            ps = next_bank()
             nc.tensor.matmul_mx(
                 out=ps[:],
                 lhsT=g_codes[g][:, t, :].bitcast(E5M2),
@@ -190,7 +199,7 @@ def tile_chebyshev_l3_sparsed32_stack_pb_v_kernel(
             )
 
         def dpt_transpose(g, t):
-            ps = banks.tile([P, 2, 2, P], F32, name="bank")
+            ps = next_bank().rearrange("p (a u m) -> p a u m", a=2, u=2)
             words = dp_flat[g][:, K * t : K * (t + 1)].bitcast(F32)
             for h in range(2):
                 for u in range(2):
@@ -233,7 +242,10 @@ def tile_chebyshev_l3_sparsed32_stack_pb_v_kernel(
             quantize(dpa_codes[g][:, n], dpa_scales[g][:, n], dpa_il[g][:, n, :].rearrange("p n t -> p (n t)"), E5M2)
 
         def interleave(engine, il, rows):
-            copy(engine, il.rearrange("p (c i) t -> p c t i", i=4), rows.rearrange("p t (c i) -> p c t i", i=4))
+            if engine == "G":
+                copy(engine, il, rows.rearrange("p t c -> p c t"))
+            else:
+                copy(engine, il.rearrange("p (c i) t -> p c t i", i=4), rows.rearrange("p t (c i) -> p c t i", i=4))
 
         def m_multiply(h):
             nc.vector.tensor_tensor(
@@ -264,7 +276,7 @@ def tile_chebyshev_l3_sparsed32_stack_pb_v_kernel(
             quantize(z_codes[g][:, n], z_scales[g][:, n], z_il[g][:, n, :].rearrange("p n t -> p (n t)"), E4M3)
 
         def product_0(g, t, w):
-            ps = banks.tile([P, N], F32, name="bank")
+            ps = next_bank()
             for h in range(2):
                 n = slice(SPAN * h + N * w, SPAN * h + N * (w + 1))
                 nc.tensor.matmul_mx(
@@ -291,7 +303,7 @@ def tile_chebyshev_l3_sparsed32_stack_pb_v_kernel(
 
         def product_1(i):
             base = window(i)
-            ps = banks.tile([P, N], F32, name="bank")
+            ps = next_bank()
             for g in range(GROUPS):
                 nc.tensor.matmul_mx(
                     out=ps[:],
@@ -328,7 +340,8 @@ def tile_chebyshev_l3_sparsed32_stack_pb_v_kernel(
                 nc.vector.memset(rows[:, 2:4, 0 : SPAN - WIN2], 0.0)
             nc.vector.memset(m_codes[:, SPAN:W], 0)
             nc.vector.memset(m_scales[:, SPAN:W].bitcast(U32), 0)
-            nc.vector.memset(zeros[:], 0.0)
+            for first in (32, 64):
+                nc.vector.memset(zeros[first : first + 32, :], 0.0)
 
         with tc.manual_schedule():
 

@@ -44,7 +44,9 @@ def tile_chebyshev_l3_sparsed32_stack_pb_v_kernel(
         U_STEP = 2 * SPAN + 2 * SHIFT
         t3_raw = [keep.tile([P, 2 * U_STEP], BF16, name="t3_raw%d" % h) for h in range(2)]
         mask_t = keep.tile([P, 2, WIN2], BF16, name="mask_t")
-        mask_o = keep.tile([P, WIN1], BF16, name="mask_o")
+        mask_row = keep.tile([P, WIN1 + 2 * SHIFT], BF16, name="mask_row")
+        mask_o = mask_row[:, SHIFT : SHIFT + WIN1]
+        picks = keep.tile([P, 2, 2, P], BF16, name="picks")
         ident = keep.tile([P, P], F32, name="ident")
         zeros = keep.tile([P, W - WIN1], F32, name="zeros")
 
@@ -72,7 +74,6 @@ def tile_chebyshev_l3_sparsed32_stack_pb_v_kernel(
         x2_v = x2.rearrange("(g p j) k -> g p j k", g=GROUPS, j=T)
         z_v = z.rearrange("(g p j) w -> g p j w", g=GROUPS, j=T)
         t3_v = T3.rearrange("(s c r) w -> c s r w", s=16, c=4, r=16)
-        mask_v = mask.rearrange("(s c r) w -> c s r w", s=16, c=4, r=16)
         mask_i = mask.rearrange("(s i j) w -> i s j w", s=16, i=8, j=8)
         out0_v = out_0.rearrange("(g p t) w -> g t p w", g=GROUPS, t=T)
         out1_v = out_1.rearrange("(s i j) w -> i s j w", s=16, i=8, j=8)
@@ -80,8 +81,8 @@ def tile_chebyshev_l3_sparsed32_stack_pb_v_kernel(
         psum = {}
         taken = []
 
-        def next_bank():
-            taken.append(banks.tile([P, N], F32, name="bank%d" % (len(taken) % 8)))
+        def next_bank(width=N, dtype=F32):
+            taken.append(banks.tile([P, width], dtype, name="bank%d" % (len(taken) % 8)))
             return taken[-1][:]
 
         sbuf = {}
@@ -121,11 +122,35 @@ def tile_chebyshev_l3_sparsed32_stack_pb_v_kernel(
                 col = 2 * SHIFT * (2 * h + u)
                 nc.sync.dma_start(out=t3_windows(h)[:, u], in_=t3_v[2 * h + u, :, :, col : col + WIN2])
 
-        def load_mask():
-            nc.sync.dma_start(out=mask_t[:], in_=mask_v[0, :, :, 0:WIN2])
+        def make_picks():
+            for first in (0, SHIFT + WIN1):
+                nc.vector.memset(mask_row[:, first : first + SHIFT], 0.0)
+            nc.vector.memset(picks[:], 0.0)
+            for l in range(2):
+                nc.vector.tensor_copy(
+                    out=picks[:, :, l].rearrange("p e (s a q) -> p e s a q", a=2, q=4)[:, :, :, l],
+                    in_=ident[:].rearrange("p (s q e) -> p e s q", q=4, e=2),
+                )
+
+        def spread_mask():
+            ps = next_bank(2 * WIN2, BF16).rearrange("p (e c) -> p e c", e=2)
+            for e in range(2):
+                for l in range(2):
+                    first = SHIFT * (1 - l)
+                    nc.tensor.matmul(
+                        out=ps[:, e],
+                        lhsT=picks[:, e, l],
+                        rhs=mask_row[:, first : first + WIN2],
+                        start=(l == 0),
+                        stop=(l == 1),
+                    )
+            psum["mask"] = ps
+
+        def mask_copy():
+            nc.vector.tensor_copy(out=mask_t[:], in_=psum["mask"])
 
         def load_mask_o():
-            nc.sync.dma_start(out=mask_o[:], in_=mask_i[0, :, :, 0:WIN1])
+            nc.sync.dma_start(out=mask_o, in_=mask_i[0, :, :, 0:WIN1])
 
         def store_0(g, t):
             nc.sync.dma_start(out=out0_v[g, t], in_=sbuf["res0", g, t][:])
@@ -134,15 +159,12 @@ def tile_chebyshev_l3_sparsed32_stack_pb_v_kernel(
             first = SHIFT * i
             nc.sync.dma_start(out=out1_v[i, :, :, first : first + WIN1], in_=sbuf["res1", i][:])
 
-        def zero_rows(width):
-            return zeros[32:96, 0:width].unsqueeze(1).to_broadcast([64, 2, width])
-
         def zero_1(i):
             left, right = SHIFT * i, W - WIN1 - SHIFT * i
             if left > 0:
-                nc.sync.dma_start(out=out1_v[i, :, :, 0:left], in_=zero_rows(left))
+                nc.sync.dma_start(out=out1_v[i, :, :, 0:left], in_=zeros[:, 0:left])
             if right > 0:
-                nc.sync.dma_start(out=out1_v[i, :, :, left + WIN1 : W], in_=zero_rows(right))
+                nc.sync.dma_start(out=out1_v[i, :, :, left + WIN1 : W], in_=zeros[:, 0:right])
 
         def g_transpose(g, b):
             ps = next_bank().rearrange("p (a u m) -> p a u m", a=2, u=2)
@@ -301,25 +323,28 @@ def tile_chebyshev_l3_sparsed32_stack_pb_v_kernel(
                 return first // N * N
             return first // 64 * 64
 
-        def product_1(i):
+        def pass_1(i, g):
             base = window(i)
-            ps = next_bank()
+            if g == 0:
+                psum["o1", i] = next_bank()
+            nc.tensor.matmul_mx(
+                out=psum["o1", i],
+                lhsT=dpa_codes[g][:, P * i : P * (i + 1)].bitcast(E5M2),
+                lhsT_scale=dpa_scales[g][:, P * i : P * (i + 1)],
+                rhs=z_codes[g][:, base : base + N].bitcast(E4M3),
+                rhs_scale=z_scales[g][:, base : base + N],
+                start=(g == 0),
+                stop=(g == GROUPS - 1),
+            )
+
+        def product_1(i):
             for g in range(GROUPS):
-                nc.tensor.matmul_mx(
-                    out=ps[:],
-                    lhsT=dpa_codes[g][:, P * i : P * (i + 1)].bitcast(E5M2),
-                    lhsT_scale=dpa_scales[g][:, P * i : P * (i + 1)],
-                    rhs=z_codes[g][:, base : base + N].bitcast(E4M3),
-                    rhs_scale=z_scales[g][:, base : base + N],
-                    start=(g == 0),
-                    stop=(g == GROUPS - 1),
-                )
-            psum["o1", i] = ps
+                pass_1(i, g)
 
         def result_1(i):
             first = SHIFT * i - window(i)
             res1 = stage.tile([P, WIN1], F32, name="res1", bufs=8)
-            nc.vector.tensor_tensor(out=res1[:], in0=psum["o1", i][:, first : first + WIN1], in1=mask_o[:], op=MULT)
+            nc.vector.tensor_tensor(out=res1[:], in0=psum["o1", i][:, first : first + WIN1], in1=mask_o, op=MULT)
             sbuf["res1", i] = res1
 
         def out_0_tile(g, t, engines="SS"):
@@ -338,10 +363,9 @@ def tile_chebyshev_l3_sparsed32_stack_pb_v_kernel(
                 rows = t3_rows(h)
                 nc.vector.memset(rows[:, 0:2, WIN2:SPAN], 0.0)
                 nc.vector.memset(rows[:, 2:4, 0 : SPAN - WIN2], 0.0)
-            nc.vector.memset(m_codes[:, SPAN:W], 0)
-            nc.vector.memset(m_scales[:, SPAN:W].bitcast(U32), 0)
-            for first in (32, 64):
-                nc.vector.memset(zeros[first : first + 32, :], 0.0)
+            nc.gpsimd.memset(m_codes[:, SPAN:W], 0)
+            nc.gpsimd.memset(m_scales[:, SPAN:W].bitcast(U32), 0)
+            nc.gpsimd.memset(zeros[:], 0.0)
 
         with tc.manual_schedule():
 
@@ -371,11 +395,12 @@ def tile_chebyshev_l3_sparsed32_stack_pb_v_kernel(
                 store_1(i)
 
             make_identity(nc, ident[:])
+            make_picks()
             fill_zeros()
+            load_mask_o()
             load_g(0, 0)
             load_cw()
             load_g(0, 1)
-            load_mask()
             load_t3(0)
             load_x2(0, 0)
             load_t3(1)
@@ -386,15 +411,16 @@ def tile_chebyshev_l3_sparsed32_stack_pb_v_kernel(
             load_x2(1, 0)
             load_x2(1, 1)
             load_z(1)
-            load_mask_o()
 
-            g_turn(0, 0)
+            spread_mask()
+            mask_copy()
             cw_copy(0, 0, 0, 16, "V")
             cw_copy(0, 1, 0, 5, "V")
             cw_copy(0, 1, 5, 16, "S")
-            g_quantize(0, 0)
+            g_turn(0, 0)
             cw_copy(1, 0, 0, 8, "V")
             cw_quantize(0)
+            g_quantize(0, 0)
             cw_copy(1, 0, 8, 16, "S")
             g_turn(0, 1)
             cw_copy(1, 1, 0, 16, "S")
@@ -475,18 +501,17 @@ def tile_chebyshev_l3_sparsed32_stack_pb_v_kernel(
             dpa_quantize(1, 0)
             z_quantize(0, 1)
             z_quantize(1, 1)
-            for t in range(3):
+            for t in range(T):
                 products_0(1, t)
                 results_0(1, t)
-            for c in range(2, 4):
-                dpa_copy(1, c, "V")
+            dpa_copy(1, 2, "V")
+            dpa_copy(1, 3, "V")
             dpa_quantize(0, 1)
             dpa_quantize(1, 1)
-            for i in range(2):
+            for i in range(4):
                 product_1(i)
-            products_0(1, 3)
-            results_0(1, 3)
-            finish_1(0)
-            finish_1(1)
-            for i in range(2, 8):
-                out_1_tile(i)
+            for g in range(GROUPS):
+                for i in range(4, 8):
+                    pass_1(i, g)
+            for i in range(8):
+                finish_1(i)

@@ -78,6 +78,8 @@ def tile_chebyshev_l3_sparsed32_stack_pb_v_kernel(
         out0_v = out_0.rearrange("(g p t) w -> g t p w", g=GROUPS, t=T)
         out1_v = out_1.rearrange("(s i j) w -> i s j w", s=16, i=8, j=8)
 
+        out1_flat = out_1.rearrange("(s r) w -> s (r w)", s=16)
+
         psum = {}
         taken = []
 
@@ -160,11 +162,15 @@ def tile_chebyshev_l3_sparsed32_stack_pb_v_kernel(
             nc.sync.dma_start(out=out1_v[i, :, :, first : first + WIN1], in_=sbuf["res1", i][:])
 
         def zero_1(i):
-            left, right = SHIFT * i, W - WIN1 - SHIFT * i
-            if left > 0:
-                nc.sync.dma_start(out=out1_v[i, :, :, 0:left], in_=zeros[:, 0:left])
-            if right > 0:
-                nc.sync.dma_start(out=out1_v[i, :, :, left + WIN1 : W], in_=zeros[:, 0:right])
+            rows = 8 if i < 7 else 7
+            first = (8 * W + SHIFT) * i + WIN1
+            runs = out1_flat[:, first : first + rows * W].rearrange("s (j w) -> s j w", j=rows)
+            nc.sync.dma_start(out=runs[:, :, 0 : W - WIN1], in_=zeros[0 : 16 * rows, :])
+
+        def zero_rest():
+            step = 8 * W + SHIFT
+            runs = out1_flat[:, 0 : 7 * step].rearrange("s (i w) -> s i w", i=7)
+            nc.sync.dma_start(out=runs[:, :, 8 * W : step], in_=zeros[0:112, 0:SHIFT])
 
         def g_transpose(g, b):
             ps = next_bank().rearrange("p (a u m) -> p a u m", a=2, u=2)
@@ -457,6 +463,7 @@ def tile_chebyshev_l3_sparsed32_stack_pb_v_kernel(
                 dpa_copy(0, c, "G")
             for i in range(5):
                 zero_1(i)
+            zero_rest()
             for t in range(2):
                 for h in range(2):
                     dx3(1, t, h)

@@ -413,6 +413,7 @@ def tile_chebyshev_l3_sparsed32_stack_pb_v_kernel(
             load_x2(0, 1)
             load_g(1, 0)
             load_g(1, 1)
+            zero_rest()
             load_z(0)
             load_x2(1, 0)
             load_x2(1, 1)
@@ -463,7 +464,6 @@ def tile_chebyshev_l3_sparsed32_stack_pb_v_kernel(
                 dpa_copy(0, c, "G")
             for i in range(5):
                 zero_1(i)
-            zero_rest()
             for t in range(2):
                 for h in range(2):
                     dx3(1, t, h)

@@ -265,8 +265,8 @@ def tile_chebyshev_l3_sparsed32_stack_pb_v_kernel(
                         src.rearrange("p t (s l q i) -> p l s q t i", l=2, q=2, i=4)[:, l],
                     )
 
-        def dpa_quantize(g, h):
-            n = slice(N * h, N * (h + 1))
+        def dpa_quantize(g, c0, c1):
+            n = slice(256 * c0, 256 * c1)
             quantize(dpa_codes[g][:, n], dpa_scales[g][:, n], dpa_il[g][:, n, :].rearrange("p n t -> p (n t)"), E5M2)
 
         def interleave(engine, il, rows):
@@ -299,8 +299,8 @@ def tile_chebyshev_l3_sparsed32_stack_pb_v_kernel(
         def z_copy(g, a, b, engine):
             interleave(engine, z_il[g][:, a:b, :], z_raw[g][:, :, a:b])
 
-        def z_quantize(g, b):
-            n = slice(N * b, N * (b + 1))
+        def z_quantize(g, a, b):
+            n = slice(a, b)
             quantize(z_codes[g][:, n], z_scales[g][:, n], z_il[g][:, n, :].rearrange("p n t -> p (n t)"), E4M3)
 
         def product_0(g, t, w):
@@ -324,14 +324,11 @@ def tile_chebyshev_l3_sparsed32_stack_pb_v_kernel(
             copy(engine, sbuf["res0", g, t][:, N * w : N * (w + 1)], psum["o0", g, t, w][:])
 
         def window(i):
-            first = SHIFT * i
-            if first + WIN1 <= N or first >= N:
-                return first // N * N
-            return first // 64 * 64
+            return (0, 0, 128, 128, 256, 384, 512, 512)[i]
 
-        def pass_1(i, g):
+        def pass_1(i, g, first=0):
             base = window(i)
-            if g == 0:
+            if g == first:
                 psum["o1", i] = next_bank()
             nc.tensor.matmul_mx(
                 out=psum["o1", i],
@@ -339,8 +336,8 @@ def tile_chebyshev_l3_sparsed32_stack_pb_v_kernel(
                 lhsT_scale=dpa_scales[g][:, P * i : P * (i + 1)],
                 rhs=z_codes[g][:, base : base + N].bitcast(E4M3),
                 rhs_scale=z_scales[g][:, base : base + N],
-                start=(g == 0),
-                stop=(g == GROUPS - 1),
+                start=(g == first),
+                stop=(g != first),
             )
 
         def product_1(i):
@@ -471,6 +468,7 @@ def tile_chebyshev_l3_sparsed32_stack_pb_v_kernel(
             products_0(0, 0)
             results_0(0, 0)
             zero_1(5)
+            zero_1(6)
             for t in range(2):
                 for h in range(2):
                     dp3(1, t, h)
@@ -482,12 +480,10 @@ def tile_chebyshev_l3_sparsed32_stack_pb_v_kernel(
             turn(1, 1)
             products_0(0, 1)
             results_0(0, 1)
-            zero_1(6)
             zero_1(7)
             for t in range(2, 4):
                 for h in range(2):
                     dp3(1, t, h)
-            z_copy(0, 768, 1024, "S")
             turn(1, 2)
             turn(1, 3)
             products_0(0, 2)
@@ -495,30 +491,38 @@ def tile_chebyshev_l3_sparsed32_stack_pb_v_kernel(
             z_copy(1, 0, 512, "V")
             dpt_quantize(1, 0)
             dpt_quantize(1, 1)
-            z_quantize(0, 0)
+            z_quantize(0, 0, 512)
             for c in range(2):
                 dpa_copy(1, c, "V")
             dpt_quantize(1, 2)
             dpt_quantize(1, 3)
             products_0(0, 3)
             results_0(0, 3)
-            z_quantize(1, 0)
-            dpa_quantize(0, 0)
+            z_quantize(1, 0, 512)
+            dpa_quantize(0, 0, 2)
             z_copy(1, 512, 1024, "V")
-            dpa_quantize(1, 0)
-            z_quantize(0, 1)
-            z_quantize(1, 1)
+            dpa_quantize(1, 0, 2)
+            z_quantize(0, 512, 768)
+            z_quantize(1, 512, 1024)
             for t in range(T):
                 products_0(1, t)
                 results_0(1, t)
+            dpa_copy(1, 3, "S")
+            z_copy(0, 768, 1024, "S")
             dpa_copy(1, 2, "V")
-            dpa_copy(1, 3, "V")
-            dpa_quantize(0, 1)
-            dpa_quantize(1, 1)
             for i in range(4):
                 product_1(i)
-            for g in range(GROUPS):
-                for i in range(4, 8):
-                    pass_1(i, g)
-            for i in range(8):
+            dpa_quantize(0, 2, 4)
+            dpa_quantize(1, 2, 3)
+            product_1(4)
+            finish_1(0)
+            finish_1(1)
+            dpa_quantize(1, 3, 4)
+            for i in range(5, 8):
+                pass_1(i, 1, first=1)
+            finish_1(2)
+            z_quantize(0, 768, 1024)
+            for i in range(5, 8):
+                pass_1(i, 0, first=1)
+            for i in range(3, 8):
                 finish_1(i)

@@ -22,6 +22,35 @@ SPAN = 640
 WIN2 = 448
 WIN1 = 352
 SHIFT = 96
+FILL = (0, 7, 1, 6, 2, 5, 3, 4)
+NARROW = (3, 4, 5, 6)
+
+
+def stored_zeros(i):
+    left, right = SHIFT * i, W - WIN1 - SHIFT * i
+    if i in NARROW:
+        return 0, 0
+    return (left, 0) if left < right else (0, right)
+
+
+def lay_out_row1():
+    order = [i for k in range(4) for i in (k, 7 - k)]
+    place, gaps, col = {}, [], 0
+    for n, i in enumerate(order):
+        place[i] = col
+        col = col + WIN1
+        gap = stored_zeros(i)[1]
+        if n + 1 < len(order):
+            gap = max(gap, stored_zeros(order[n + 1])[0])
+        if n == 0:
+            gap = W - WIN1
+        if gap > 0:
+            gaps.append((col, gap))
+        col = col + gap
+    return place, gaps, col
+
+
+PLACE, GAPS, ROW1 = lay_out_row1()
 
 FLOPS = 2 * (B * O * K + 2 * B * K * W)
 BYTES = 2 * (4 * 1024 * 1024 + 2 * 512 * 1024) + 4 * 2 * 1024 * 1024
@@ -38,7 +67,9 @@ def tile_chebyshev_l3_sparsed32_stack_pb_v_kernel(
         banks = ctx.enter_context(tc.psum_pool(name="banks", bufs=1))
 
         cw_raw = keep.tile([P, T, K], BF16, name="cw_raw")
-        g_raw = [[keep.tile([P, 2, O], BF16, name="g_raw%d%d" % (g, b)) for b in range(2)] for g in range(GROUPS)]
+        g_first = [keep.tile([P, 2, O], BF16, name="g_first%d" % b) for b in range(2)]
+        g_second = keep.tile([P, T, O], BF16, name="g_second")
+        g_raw = [[g_first[b][:] for b in range(2)], [g_second[:, 2 * b : 2 * b + 2] for b in range(2)]]
         x2_raw = [[keep.tile([P, 2, K], BF16, name="x2_raw%d%d" % (g, b)) for b in range(2)] for g in range(GROUPS)]
         z_raw = [keep.tile([P, T, W], BF16, name="z_raw%d" % g) for g in range(GROUPS)]
         U_STEP = 2 * SPAN + 2 * SHIFT
@@ -48,7 +79,7 @@ def tile_chebyshev_l3_sparsed32_stack_pb_v_kernel(
         mask_o = mask_row[:, SHIFT : SHIFT + WIN1]
         picks = keep.tile([P, 2, 2, P], BF16, name="picks")
         ident = keep.tile([P, P], F32, name="ident")
-        zeros = keep.tile([P, W - WIN1], F32, name="zeros")
+        row1 = keep.tile([P, ROW1], F32, name="row1")
 
         cw_il = keep.tile([P, 2, N, T], BF16, name="cw_il", align_bytes=64)
         cw_codes = keep.tile([P, 2, N], U32, name="cw_codes", align_bytes=64)
@@ -77,8 +108,6 @@ def tile_chebyshev_l3_sparsed32_stack_pb_v_kernel(
         mask_i = mask.rearrange("(s i j) w -> i s j w", s=16, i=8, j=8)
         out0_v = out_0.rearrange("(g p t) w -> g t p w", g=GROUPS, t=T)
         out1_v = out_1.rearrange("(s i j) w -> i s j w", s=16, i=8, j=8)
-
-        out1_flat = out_1.rearrange("(s r) w -> s (r w)", s=16)
 
         psum = {}
         taken = []
@@ -110,8 +139,11 @@ def tile_chebyshev_l3_sparsed32_stack_pb_v_kernel(
         def load_cw():
             nc.sync.dma_start(out=cw_raw[:], in_=cw_v)
 
-        def load_g(g, b):
-            nc.sync.dma_start(out=g_raw[g][b][:], in_=g_v[g, :, 2 * b : 2 * b + 2])
+        def load_g_first(b):
+            nc.sync.dma_start(out=g_first[b][:], in_=g_v[0, :, 2 * b : 2 * b + 2])
+
+        def load_g_second():
+            nc.sync.dma_start(out=g_second[:], in_=g_v[1])
 
         def load_x2(g, b):
             nc.sync.dma_start(out=x2_raw[g][b][:], in_=x2_v[g, :, 2 * b : 2 * b + 2])
@@ -154,23 +186,23 @@ def tile_chebyshev_l3_sparsed32_stack_pb_v_kernel(
         def load_mask_o():
             nc.sync.dma_start(out=mask_o, in_=mask_i[0, :, :, 0:WIN1])
 
-        def store_0(g, t):
-            nc.sync.dma_start(out=out0_v[g, t], in_=sbuf["res0", g, t][:])
+        def store_0(g, t, queue=nc.sync):
+            queue.dma_start(out=out0_v[g, t], in_=sbuf["res0", g, t][:])
 
         def store_1(i):
+            left, right = stored_zeros(i)
             first = SHIFT * i
-            nc.sync.dma_start(out=out1_v[i, :, :, first : first + WIN1], in_=sbuf["res1", i][:])
+            nc.sync.dma_start(
+                out=out1_v[i, :, :, first - left : first + WIN1 + right],
+                in_=row1[:, PLACE[i] - left : PLACE[i] + WIN1 + right],
+            )
 
         def zero_1(i):
-            rows = 8 if i < 7 else 7
-            first = (8 * W + SHIFT) * i + WIN1
-            runs = out1_flat[:, first : first + rows * W].rearrange("s (j w) -> s j w", j=rows)
-            nc.sync.dma_start(out=runs[:, :, 0 : W - WIN1], in_=zeros[0 : 16 * rows, :])
-
-        def zero_rest():
-            step = 8 * W + SHIFT
-            runs = out1_flat[:, 0 : 7 * step].rearrange("s (i w) -> s i w", i=7)
-            nc.sync.dma_start(out=runs[:, :, 8 * W : step], in_=zeros[0:112, 0:SHIFT])
+            left, right = SHIFT * i, W - WIN1 - SHIFT * i
+            if left > right or i in NARROW:
+                nc.sync.dma_start(out=out1_v[i, :, :, 0:left], in_=row1[:, WIN1 : WIN1 + left])
+            if left < right or i in NARROW:
+                nc.sync.dma_start(out=out1_v[i, :, :, left + WIN1 : W], in_=row1[:, WIN1 : WIN1 + right])
 
         def g_transpose(g, b):
             ps = next_bank().rearrange("p (a u m) -> p a u m", a=2, u=2)
@@ -346,20 +378,12 @@ def tile_chebyshev_l3_sparsed32_stack_pb_v_kernel(
 
         def result_1(i):
             first = SHIFT * i - window(i)
-            res1 = stage.tile([P, WIN1], F32, name="res1", bufs=8)
-            nc.vector.tensor_tensor(out=res1[:], in0=psum["o1", i][:, first : first + WIN1], in1=mask_o, op=MULT)
-            sbuf["res1", i] = res1
-
-        def out_0_tile(g, t, engines="SS"):
-            for w in range(2):
-                product_0(g, t, w)
-                result_0(g, t, w, engines[w])
-            store_0(g, t)
-
-        def out_1_tile(i):
-            product_1(i)
-            result_1(i)
-            store_1(i)
+            nc.vector.tensor_tensor(
+                out=row1[:, PLACE[i] : PLACE[i] + WIN1],
+                in0=psum["o1", i][:, first : first + WIN1],
+                in1=mask_o,
+                op=MULT,
+            )
 
         def fill_zeros():
             for h in range(2):
@@ -368,7 +392,9 @@ def tile_chebyshev_l3_sparsed32_stack_pb_v_kernel(
                 nc.vector.memset(rows[:, 2:4, 0 : SPAN - WIN2], 0.0)
             nc.gpsimd.memset(m_codes[:, SPAN:W], 0)
             nc.gpsimd.memset(m_scales[:, SPAN:W].bitcast(U32), 0)
-            nc.gpsimd.memset(zeros[:], 0.0)
+            for n, (first, width) in enumerate(GAPS):
+                engine = nc.gpsimd if n == 0 else nc.vector
+                engine.memset(row1[:, first : first + width].bitcast(U32), 0)
 
         with tc.manual_schedule():
 
@@ -391,7 +417,6 @@ def tile_chebyshev_l3_sparsed32_stack_pb_v_kernel(
             def results_0(g, t, engines="SS"):
                 for w in range(2):
                     result_0(g, t, w, engines[w])
-                store_0(g, t)
 
             def finish_1(i):
                 result_1(i)
@@ -401,20 +426,20 @@ def tile_chebyshev_l3_sparsed32_stack_pb_v_kernel(
             make_picks()
             fill_zeros()
             load_mask_o()
-            load_g(0, 0)
+            load_g_first(0)
             load_cw()
-            load_g(0, 1)
+            load_g_first(1)
             load_t3(0)
             load_x2(0, 0)
             load_t3(1)
             load_x2(0, 1)
-            load_g(1, 0)
-            load_g(1, 1)
-            zero_rest()
+            load_g_second()
             load_z(0)
             load_x2(1, 0)
             load_x2(1, 1)
             load_z(1)
+            for i in FILL[:5]:
+                zero_1(i)
 
             spread_mask()
             mask_copy()
@@ -459,16 +484,15 @@ def tile_chebyshev_l3_sparsed32_stack_pb_v_kernel(
                 dpt_quantize(0, t)
             for c in (2, 3, 1):
                 dpa_copy(0, c, "G")
-            for i in range(5):
-                zero_1(i)
             for t in range(2):
                 for h in range(2):
                     dx3(1, t, h)
             z_copy(0, 0, 512, "S")
             products_0(0, 0)
             results_0(0, 0)
-            zero_1(5)
-            zero_1(6)
+            store_0(0, 0)
+            for i in FILL[5:7]:
+                zero_1(i)
             for t in range(2):
                 for h in range(2):
                     dp3(1, t, h)
@@ -480,7 +504,8 @@ def tile_chebyshev_l3_sparsed32_stack_pb_v_kernel(
             turn(1, 1)
             products_0(0, 1)
             results_0(0, 1)
-            zero_1(7)
+            store_0(0, 1)
+            zero_1(FILL[7])
             for t in range(2, 4):
                 for h in range(2):
                     dp3(1, t, h)
@@ -488,6 +513,7 @@ def tile_chebyshev_l3_sparsed32_stack_pb_v_kernel(
             turn(1, 3)
             products_0(0, 2)
             results_0(0, 2)
+            store_0(0, 2)
             z_copy(1, 0, 512, "V")
             dpt_quantize(1, 0)
             dpt_quantize(1, 1)
@@ -504,10 +530,22 @@ def tile_chebyshev_l3_sparsed32_stack_pb_v_kernel(
             dpa_quantize(1, 0, 2)
             z_quantize(0, 512, 768)
             z_quantize(1, 512, 1024)
-            for t in range(T):
-                products_0(1, t)
-                results_0(1, t)
+            products_0(1, 0)
+            result_0(1, 0, 0)
+            store_0(0, 3, nc.scalar)
+            result_0(1, 0, 1)
+            store_0(1, 0)
+            products_0(1, 1)
+            results_0(1, 1)
+            products_0(1, 2)
+            result_0(1, 2, 0)
+            store_0(1, 1, nc.scalar)
+            result_0(1, 2, 1)
+            store_0(1, 2)
+            products_0(1, 3)
+            results_0(1, 3)
             dpa_copy(1, 3, "S")
+            store_0(1, 3, nc.scalar)
             z_copy(0, 768, 1024, "S")
             dpa_copy(1, 2, "V")
             for i in range(4):

@@ -19,9 +19,10 @@ GROUPS = 2
 T = 4
 N = 512
 SPAN = 640
-WIN2 = 448
 WIN1 = 352
 SHIFT = 96
+L_STEP = 2 * SPAN + SHIFT
+U_STEP = SPAN + 2 * SHIFT
 FILL = (0, 7, 1, 6, 2, 5, 3, 4)
 NARROW = (3, 4, 5, 6)
 
@@ -72,12 +73,9 @@ def tile_chebyshev_l3_sparsed32_stack_pb_v_kernel(
         g_raw = [[g_first[b][:] for b in range(2)], [g_second[:, 2 * b : 2 * b + 2] for b in range(2)]]
         x2_raw = [[keep.tile([P, 2, K], BF16, name="x2_raw%d%d" % (g, b)) for b in range(2)] for g in range(GROUPS)]
         z_raw = [keep.tile([P, T, W], BF16, name="z_raw%d" % g) for g in range(GROUPS)]
-        U_STEP = 2 * SPAN + 2 * SHIFT
-        t3_raw = [keep.tile([P, 2 * U_STEP], BF16, name="t3_raw%d" % h) for h in range(2)]
-        mask_t = keep.tile([P, 2, WIN2], BF16, name="mask_t")
-        mask_row = keep.tile([P, WIN1 + 2 * SHIFT], BF16, name="mask_row")
-        mask_o = mask_row[:, SHIFT : SHIFT + WIN1]
-        picks = keep.tile([P, 2, 2, P], BF16, name="picks")
+        t3_raw = [keep.tile([P, L_STEP + 2 * U_STEP], BF16, name="t3_raw%d" % h) for h in range(2)]
+        mask_row = keep.tile([P, WIN1], BF16, name="mask_row")
+        mask_o = mask_row[:]
         ident = keep.tile([P, P], F32, name="ident")
         row1 = keep.tile([P, ROW1], F32, name="row1")
 
@@ -104,7 +102,7 @@ def tile_chebyshev_l3_sparsed32_stack_pb_v_kernel(
         g_v = grad_out.rearrange("(g p j) o -> g p j o", g=GROUPS, j=T)
         x2_v = x2.rearrange("(g p j) k -> g p j k", g=GROUPS, j=T)
         z_v = z.rearrange("(g p j) w -> g p j w", g=GROUPS, j=T)
-        t3_v = T3.rearrange("(s c r) w -> c s r w", s=16, c=4, r=16)
+        t3_v = T3.rearrange("(s i j) w -> i s j w", s=16, i=8, j=8)
         mask_i = mask.rearrange("(s i j) w -> i s j w", s=16, i=8, j=8)
         out0_v = out_0.rearrange("(g p t) w -> g t p w", g=GROUPS, t=T)
         out1_v = out_1.rearrange("(s i j) w -> i s j w", s=16, i=8, j=8)
@@ -129,9 +127,9 @@ def tile_chebyshev_l3_sparsed32_stack_pb_v_kernel(
         def quantize(codes, scales, values, fmt):
             nc.vector.quantize_mx(out=codes.bitcast(fmt), scales=scales, in_=values)
 
-        def t3_windows(h):
-            by_u = t3_raw[h][:].rearrange("p (u x) -> p u x", u=2)[:, :, 0 : 2 * SPAN]
-            return by_u.rearrange("p u (e c) -> p u e c", e=2)[:, :, :, 0:WIN2]
+        def t3_windows(h, l):
+            by_u = t3_raw[h][:, L_STEP * l : L_STEP * l + 2 * U_STEP]
+            return by_u.rearrange("p (u c) -> p u c", u=2)[:, :, 0:WIN1]
 
         def t3_rows(h):
             return t3_raw[h][:, 0 : T * SPAN].rearrange("p (t c) -> p t c", t=T)
@@ -152,42 +150,16 @@ def tile_chebyshev_l3_sparsed32_stack_pb_v_kernel(
             nc.sync.dma_start(out=z_raw[g][:], in_=z_v[g])
 
         def load_t3(h):
-            for u in range(2):
-                col = 2 * SHIFT * (2 * h + u)
-                nc.sync.dma_start(out=t3_windows(h)[:, u], in_=t3_v[2 * h + u, :, :, col : col + WIN2])
-
-        def make_picks():
-            for first in (0, SHIFT + WIN1):
-                nc.vector.memset(mask_row[:, first : first + SHIFT], 0.0)
-            nc.vector.memset(picks[:], 0.0)
             for l in range(2):
-                nc.vector.tensor_copy(
-                    out=picks[:, :, l].rearrange("p e (s a q) -> p e s a q", a=2, q=4)[:, :, :, l],
-                    in_=ident[:].rearrange("p (s q e) -> p e s q", q=4, e=2),
-                )
-
-        def spread_mask():
-            ps = next_bank(2 * WIN2, BF16).rearrange("p (e c) -> p e c", e=2)
-            for e in range(2):
-                for l in range(2):
-                    first = SHIFT * (1 - l)
-                    nc.tensor.matmul(
-                        out=ps[:, e],
-                        lhsT=picks[:, e, l],
-                        rhs=mask_row[:, first : first + WIN2],
-                        start=(l == 0),
-                        stop=(l == 1),
-                    )
-            psum["mask"] = ps
-
-        def mask_copy():
-            nc.vector.tensor_copy(out=mask_t[:], in_=psum["mask"])
+                for u in range(2):
+                    i = 4 * h + 2 * u + l
+                    nc.sync.dma_start(out=t3_windows(h, l)[:, u], in_=t3_v[i, :, :, SHIFT * i : SHIFT * i + WIN1])
 
         def load_mask_o():
             nc.sync.dma_start(out=mask_o, in_=mask_i[0, :, :, 0:WIN1])
 
-        def store_0(g, t, queue=nc.sync):
-            queue.dma_start(out=out0_v[g, t], in_=sbuf["res0", g, t][:])
+        def store_0(g, t):
+            nc.sync.dma_start(out=out0_v[g, t], in_=sbuf["res0", g, t][:])
 
         def store_1(i):
             left, right = stored_zeros(i)
@@ -250,10 +222,10 @@ def tile_chebyshev_l3_sparsed32_stack_pb_v_kernel(
             psum["dx", g, t, h] = ps
 
         def dp3(g, t, h):
-            x2_p = x2_raw[g][t // 2][:, t % 2, :].rearrange("p (s h u r) -> p h u s r", s=16, h=2, u=2, r=16)
+            x2_p = x2_raw[g][t // 2][:, t % 2, :].rearrange("p (s h u l j) -> p h s l j u", s=16, h=2, u=2, l=2)
             nc.vector.tensor_tensor(
-                out=dp[g][:, t, N * h : N * (h + 1)].rearrange("p (u s r) -> p u s r", u=2, r=16),
-                in0=psum["dx", g, t, h][:].rearrange("p (u s r) -> p u s r", u=2, r=16),
+                out=dp[g][:, t, N * h : N * (h + 1)].rearrange("p (l s j u) -> p s l j u", l=2, s=16, u=2),
+                in0=psum["dx", g, t, h][:].rearrange("p (u s l j) -> p s l j u", u=2, s=16, l=2),
                 in1=x2_p[:, h],
                 op=MULT,
             )
@@ -284,18 +256,13 @@ def tile_chebyshev_l3_sparsed32_stack_pb_v_kernel(
             src = dp[g][:, :, 256 * c : 256 * (c + 1)]
             dst = dpa_il[g][:, 256 * c : 256 * (c + 1), :]
             if engine == "G":
+                copy(engine, dst.rearrange("p (u m) t -> p u m t", u=2), src.rearrange("p t (m u) -> p u m t", u=2))
+            else:
                 copy(
                     engine,
-                    dst.rearrange("p (l s j) t -> p s l j t", l=2, j=8),
-                    src.rearrange("p t (s l j) -> p s l j t", l=2, j=8),
+                    dst.rearrange("p (u m i) t -> p u m t i", u=2, i=4),
+                    src.rearrange("p t (m i u) -> p u m t i", u=2, i=4),
                 )
-            else:
-                for l in range(2):
-                    copy(
-                        engine,
-                        dst.rearrange("p (l s q i) t -> p l s q t i", l=2, q=2, i=4)[:, l],
-                        src.rearrange("p t (s l q i) -> p l s q t i", l=2, q=2, i=4)[:, l],
-                    )
 
         def dpa_quantize(g, c0, c1):
             n = slice(256 * c0, 256 * c1)
@@ -308,12 +275,13 @@ def tile_chebyshev_l3_sparsed32_stack_pb_v_kernel(
                 copy(engine, il.rearrange("p (c i) t -> p c t i", i=4), rows.rearrange("p t (c i) -> p c t i", i=4))
 
         def m_multiply(h):
-            nc.vector.tensor_tensor(
-                out=t3_windows(h),
-                in0=t3_windows(h),
-                in1=mask_t[:].unsqueeze(1).to_broadcast([P, 2, 2, WIN2]),
-                op=MULT,
-            )
+            for l in range(2):
+                nc.vector.tensor_tensor(
+                    out=t3_windows(h, l),
+                    in0=t3_windows(h, l),
+                    in1=mask_o.unsqueeze(1).to_broadcast([P, 2, WIN1]),
+                    op=MULT,
+                )
 
         def m_copy(h, a, b, engine):
             interleave(engine, m_il[h][:, a:b, :], t3_rows(h)[:, :, a:b])
@@ -360,12 +328,13 @@ def tile_chebyshev_l3_sparsed32_stack_pb_v_kernel(
 
         def pass_1(i, g, first=0):
             base = window(i)
+            col = N * (i // 4) + 256 * (i % 2) + P * (i // 2 % 2)
             if g == first:
                 psum["o1", i] = next_bank()
             nc.tensor.matmul_mx(
                 out=psum["o1", i],
-                lhsT=dpa_codes[g][:, P * i : P * (i + 1)].bitcast(E5M2),
-                lhsT_scale=dpa_scales[g][:, P * i : P * (i + 1)],
+                lhsT=dpa_codes[g][:, col : col + P].bitcast(E5M2),
+                lhsT_scale=dpa_scales[g][:, col : col + P],
                 rhs=z_codes[g][:, base : base + N].bitcast(E4M3),
                 rhs_scale=z_scales[g][:, base : base + N],
                 start=(g == first),
@@ -388,8 +357,12 @@ def tile_chebyshev_l3_sparsed32_stack_pb_v_kernel(
         def fill_zeros():
             for h in range(2):
                 rows = t3_rows(h)
-                nc.vector.memset(rows[:, 0:2, WIN2:SPAN], 0.0)
-                nc.vector.memset(rows[:, 2:4, 0 : SPAN - WIN2], 0.0)
+                for t in range(T):
+                    first = SHIFT * (2 * (t % 2) + t // 2)
+                    if first > 0:
+                        nc.vector.memset(rows[:, t, 0:first], 0.0)
+                    if first + WIN1 < SPAN:
+                        nc.vector.memset(rows[:, t, first + WIN1 : SPAN], 0.0)
             nc.gpsimd.memset(m_codes[:, SPAN:W], 0)
             nc.gpsimd.memset(m_scales[:, SPAN:W].bitcast(U32), 0)
             for n, (first, width) in enumerate(GAPS):
@@ -417,13 +390,13 @@ def tile_chebyshev_l3_sparsed32_stack_pb_v_kernel(
             def results_0(g, t, engines="SS"):
                 for w in range(2):
                     result_0(g, t, w, engines[w])
+                store_0(g, t)
 
             def finish_1(i):
                 result_1(i)
                 store_1(i)
 
             make_identity(nc, ident[:])
-            make_picks()
             fill_zeros()
             load_mask_o()
             load_g_first(0)
@@ -441,8 +414,6 @@ def tile_chebyshev_l3_sparsed32_stack_pb_v_kernel(
             for i in FILL[:5]:
                 zero_1(i)
 
-            spread_mask()
-            mask_copy()
             cw_copy(0, 0, 0, 16, "V")
             cw_copy(0, 1, 0, 5, "V")
             cw_copy(0, 1, 5, 16, "S")
@@ -490,7 +461,6 @@ def tile_chebyshev_l3_sparsed32_stack_pb_v_kernel(
             z_copy(0, 0, 512, "S")
             products_0(0, 0)
             results_0(0, 0)
-            store_0(0, 0)
             for i in FILL[5:7]:
                 zero_1(i)
             for t in range(2):
@@ -504,7 +474,6 @@ def tile_chebyshev_l3_sparsed32_stack_pb_v_kernel(
             turn(1, 1)
             products_0(0, 1)
             results_0(0, 1)
-            store_0(0, 1)
             zero_1(FILL[7])
             for t in range(2, 4):
                 for h in range(2):
@@ -513,7 +482,6 @@ def tile_chebyshev_l3_sparsed32_stack_pb_v_kernel(
             turn(1, 3)
             products_0(0, 2)
             results_0(0, 2)
-            store_0(0, 2)
             z_copy(1, 0, 512, "V")
             dpt_quantize(1, 0)
             dpt_quantize(1, 1)
@@ -530,22 +498,10 @@ def tile_chebyshev_l3_sparsed32_stack_pb_v_kernel(
             dpa_quantize(1, 0, 2)
             z_quantize(0, 512, 768)
             z_quantize(1, 512, 1024)
-            products_0(1, 0)
-            result_0(1, 0, 0)
-            store_0(0, 3, nc.scalar)
-            result_0(1, 0, 1)
-            store_0(1, 0)
-            products_0(1, 1)
-            results_0(1, 1)
-            products_0(1, 2)
-            result_0(1, 2, 0)
-            store_0(1, 1, nc.scalar)
-            result_0(1, 2, 1)
-            store_0(1, 2)
-            products_0(1, 3)
-            results_0(1, 3)
+            for t in range(T):
+                products_0(1, t)
+                results_0(1, t)
             dpa_copy(1, 3, "S")
-            store_0(1, 3, nc.scalar)
             z_copy(0, 768, 1024, "S")
             dpa_copy(1, 2, "V")
             for i in range(4):
@@ -553,10 +509,11 @@ def tile_chebyshev_l3_sparsed32_stack_pb_v_kernel(
             dpa_quantize(0, 2, 4)
             dpa_quantize(1, 2, 3)
             product_1(4)
+            pass_1(6, 1, first=1)
             finish_1(0)
             finish_1(1)
             dpa_quantize(1, 3, 4)
-            for i in range(5, 8):
+            for i in (5, 7):
                 pass_1(i, 1, first=1)
             finish_1(2)
             z_quantize(0, 768, 1024)

@@ -21,6 +21,7 @@ N = 512
 SPAN = 640
 WIN1 = 352
 SHIFT = 96
+HOLD = 2
 L_STEP = 2 * SPAN + SHIFT
 U_STEP = SPAN + 2 * SHIFT
 FILL = (0, 7, 1, 6, 2, 5, 3, 4)
@@ -64,18 +65,22 @@ def tile_chebyshev_l3_sparsed32_stack_pb_v_kernel(
     with ExitStack() as ctx:
         keep = ctx.enter_context(tc.tile_pool(name="keep", bufs=1))
         stage = ctx.enter_context(tc.tile_pool(name="stage", bufs=4))
-        stage0 = ctx.enter_context(tc.tile_pool(name="stage0", bufs=5))
+        stage0 = ctx.enter_context(tc.tile_pool(name="stage0", bufs=8))
         banks = ctx.enter_context(tc.psum_pool(name="banks", bufs=1))
 
         cw_raw = keep.tile([P, T, K], BF16, name="cw_raw")
         g_first = [keep.tile([P, 2, O], BF16, name="g_first%d" % b) for b in range(2)]
         g_second = keep.tile([P, T, O], BF16, name="g_second")
         g_raw = [[g_first[b][:] for b in range(2)], [g_second[:, 2 * b : 2 * b + 2] for b in range(2)]]
-        x2_raw = [[keep.tile([P, 2, K], BF16, name="x2_raw%d%d" % (g, b)) for b in range(2)] for g in range(GROUPS)]
+        x2_first = [keep.tile([P, 2, K], BF16, name="x2_first%d" % b) for b in range(2)]
+        x2_second = keep.tile([P, T, K], BF16, name="x2_second")
+        x2_raw = [[x2_first[b][:] for b in range(2)], [x2_second[:, 2 * b : 2 * b + 2] for b in range(2)]]
         z_raw = [keep.tile([P, T, W], BF16, name="z_raw%d" % g) for g in range(GROUPS)]
         t3_raw = [keep.tile([P, L_STEP + 2 * U_STEP], BF16, name="t3_raw%d" % h) for h in range(2)]
         mask_row = keep.tile([P, WIN1], BF16, name="mask_row")
         mask_o = mask_row[:]
+        mask_few = keep.tile([P, WIN1], BF16, name="mask_few")
+        picks = keep.tile([P, 16, 8], BF16, name="picks")
         ident = keep.tile([P, P], F32, name="ident")
         row1 = keep.tile([P, ROW1], F32, name="row1")
 
@@ -91,7 +96,7 @@ def tile_chebyshev_l3_sparsed32_stack_pb_v_kernel(
         dp = [d[:].rearrange("p (t k) -> p t k", t=T) for d in dp_flat]
         dpt_codes = [keep.tile([P, T, 2, P], U32, name="dpt_codes%d" % g, align_bytes=64) for g in range(GROUPS)]
         dpt_scales = [keep.tile([P, T, 2, P], U8, name="dpt_scales%d" % g, align_bytes=64) for g in range(GROUPS)]
-        dpa_il = [keep.tile([P, K, T], BF16, name="dpa_il%d" % g, align_bytes=64) for g in range(GROUPS)]
+        dpa_il = {}
         dpa_codes = [keep.tile([P, K], U32, name="dpa_codes%d" % g, align_bytes=64) for g in range(GROUPS)]
         dpa_scales = [keep.tile([P, K], U8, name="dpa_scales%d" % g, align_bytes=64) for g in range(GROUPS)]
         z_il = [keep.tile([P, W, T], BF16, name="z_il%d" % g, align_bytes=64) for g in range(GROUPS)]
@@ -103,7 +108,6 @@ def tile_chebyshev_l3_sparsed32_stack_pb_v_kernel(
         x2_v = x2.rearrange("(g p j) k -> g p j k", g=GROUPS, j=T)
         z_v = z.rearrange("(g p j) w -> g p j w", g=GROUPS, j=T)
         t3_v = T3.rearrange("(s i j) w -> i s j w", s=16, i=8, j=8)
-        mask_i = mask.rearrange("(s i j) w -> i s j w", s=16, i=8, j=8)
         out0_v = out_0.rearrange("(g p t) w -> g t p w", g=GROUPS, t=T)
         out1_v = out_1.rearrange("(s i j) w -> i s j w", s=16, i=8, j=8)
 
@@ -143,8 +147,11 @@ def tile_chebyshev_l3_sparsed32_stack_pb_v_kernel(
         def load_g_second():
             nc.sync.dma_start(out=g_second[:], in_=g_v[1])
 
-        def load_x2(g, b):
-            nc.sync.dma_start(out=x2_raw[g][b][:], in_=x2_v[g, :, 2 * b : 2 * b + 2])
+        def load_x2_first(b):
+            nc.sync.dma_start(out=x2_first[b][:], in_=x2_v[0, :, 2 * b : 2 * b + 2])
+
+        def load_x2_second():
+            nc.sync.dma_start(out=x2_second[:], in_=x2_v[1])
 
         def load_z(g):
             nc.sync.dma_start(out=z_raw[g][:], in_=z_v[g])
@@ -155,8 +162,22 @@ def tile_chebyshev_l3_sparsed32_stack_pb_v_kernel(
                     i = 4 * h + 2 * u + l
                     nc.sync.dma_start(out=t3_windows(h, l)[:, u], in_=t3_v[i, :, :, SHIFT * i : SHIFT * i + WIN1])
 
-        def load_mask_o():
-            nc.sync.dma_start(out=mask_o, in_=mask_i[0, :, :, 0:WIN1])
+        def load_mask():
+            nc.sync.dma_start(out=mask_few[0:8, :], in_=mask[0:8, 0:WIN1])
+
+        def prepare_mask():
+            nc.vector.memset(mask_few[:], 0.0)
+            nc.vector.tensor_copy(out=picks[:], in_=ident[:, 0:8].unsqueeze(1).to_broadcast([P, 16, 8]))
+
+        def spread_mask():
+            ps = next_bank(WIN1, BF16)
+            nc.tensor.matmul(
+                out=ps, lhsT=picks[:].rearrange("p s j -> p (s j)"), rhs=mask_few[:], start=True, stop=True
+            )
+            psum["mask"] = ps
+
+        def mask_copy():
+            nc.vector.tensor_copy(out=mask_o, in_=psum["mask"])
 
         def store_0(g, t):
             nc.sync.dma_start(out=out0_v[g, t], in_=sbuf["res0", g, t][:])
@@ -240,7 +261,10 @@ def tile_chebyshev_l3_sparsed32_stack_pb_v_kernel(
             psum["dpt", g, t] = ps
 
         def dpt_copy(g, t, engine="S"):
-            il = stage.tile([P, 2, P, 2], F32, name="words_il", align_bytes=64, bufs=6)
+            if (g, t) == (0, HOLD):
+                il = keep.tile([P, 2, P, 2], F32, name="held", align_bytes=64)
+            else:
+                il = stage.tile([P, 2, P, 2], F32, name="words_il", align_bytes=64, bufs=6)
             copy(engine, il[:], psum["dpt", g, t][:].rearrange("p h u m -> p h m u"))
             sbuf["dpt", g, t] = il
 
@@ -254,7 +278,15 @@ def tile_chebyshev_l3_sparsed32_stack_pb_v_kernel(
 
         def dpa_copy(g, c, engine):
             src = dp[g][:, :, 256 * c : 256 * (c + 1)]
-            dst = dpa_il[g][:, 256 * c : 256 * (c + 1), :]
+            if (g, c) == (0, 2):
+                dpa_il[g, c] = keep.tile([P, 256, T], BF16, name="held", align_bytes=64)[:]
+            elif (g, c) == (0, 3):
+                dpa_il[g, c] = keep.tile([P, 256, T], BF16, name="dpa_il03", align_bytes=64)[:]
+            else:
+                if (g, c // 2) not in sbuf:
+                    sbuf[g, c // 2] = keep.tile([P, N, T], BF16, name="dpa_il%d%d" % (g, c // 2), align_bytes=64)
+                dpa_il[g, c] = sbuf[g, c // 2][:, 256 * (c % 2) : 256 * (c % 2 + 1), :]
+            dst = dpa_il[g, c]
             if engine == "G":
                 copy(engine, dst.rearrange("p (u m) t -> p u m t", u=2), src.rearrange("p t (m u) -> p u m t", u=2))
             else:
@@ -266,7 +298,8 @@ def tile_chebyshev_l3_sparsed32_stack_pb_v_kernel(
 
         def dpa_quantize(g, c0, c1):
             n = slice(256 * c0, 256 * c1)
-            quantize(dpa_codes[g][:, n], dpa_scales[g][:, n], dpa_il[g][:, n, :].rearrange("p n t -> p (n t)"), E5M2)
+            values = dpa_il[g, c0] if c1 == c0 + 1 else sbuf[g, c0 // 2][:]
+            quantize(dpa_codes[g][:, n], dpa_scales[g][:, n], values.rearrange("p n t -> p (n t)"), E5M2)
 
         def interleave(engine, il, rows):
             if engine == "G":
@@ -397,19 +430,19 @@ def tile_chebyshev_l3_sparsed32_stack_pb_v_kernel(
                 store_1(i)
 
             make_identity(nc, ident[:])
+            prepare_mask()
             fill_zeros()
-            load_mask_o()
             load_g_first(0)
             load_cw()
+            load_mask()
             load_g_first(1)
             load_t3(0)
-            load_x2(0, 0)
+            load_x2_first(0)
             load_t3(1)
-            load_x2(0, 1)
+            load_x2_first(1)
             load_g_second()
             load_z(0)
-            load_x2(1, 0)
-            load_x2(1, 1)
+            load_x2_second()
             load_z(1)
             for i in FILL[:5]:
                 zero_1(i)
@@ -418,7 +451,9 @@ def tile_chebyshev_l3_sparsed32_stack_pb_v_kernel(
             cw_copy(0, 1, 0, 5, "V")
             cw_copy(0, 1, 5, 16, "S")
             g_turn(0, 0)
+            spread_mask()
             cw_copy(1, 0, 0, 8, "V")
+            mask_copy()
             cw_quantize(0)
             g_quantize(0, 0)
             cw_copy(1, 0, 8, 16, "S")
@@ -506,7 +541,8 @@ def tile_chebyshev_l3_sparsed32_stack_pb_v_kernel(
             dpa_copy(1, 2, "V")
             for i in range(4):
                 product_1(i)
-            dpa_quantize(0, 2, 4)
+            dpa_quantize(0, 2, 3)
+            dpa_quantize(0, 3, 4)
             dpa_quantize(1, 2, 3)
             product_1(4)
             pass_1(6, 1, first=1)

@@ -21,6 +21,7 @@ N = 512
 SPAN = 640
 WIN1 = 352
 SHIFT = 96
+COVER = 384
 HOLD = 2
 L_STEP = 2 * SPAN + SHIFT
 U_STEP = SPAN + 2 * SHIFT
@@ -90,8 +91,8 @@ def tile_chebyshev_l3_sparsed32_stack_pb_v_kernel(
         g_codes = [keep.tile([P, T, P], U32, name="g_codes%d" % g, align_bytes=64) for g in range(GROUPS)]
         g_scales = [keep.tile([P, T, P], U8, name="g_scales%d" % g, align_bytes=64) for g in range(GROUPS)]
         m_il = [keep.tile([P, SPAN, T], BF16, name="m_il%d" % h, align_bytes=64) for h in range(2)]
-        m_codes = keep.tile([P, SPAN + W], U32, name="m_codes", align_bytes=64)
-        m_scales = keep.tile([P, SPAN + W], U8, name="m_scales", align_bytes=64)
+        m_codes = keep.tile([P, 2 * SPAN], U32, name="m_codes", align_bytes=64)
+        m_scales = keep.tile([P, 2 * SPAN], U8, name="m_scales", align_bytes=64)
         dp_flat = [keep.tile([P, T * K], BF16, name="dp%d" % g) for g in range(GROUPS)]
         dp = [d[:].rearrange("p (t k) -> p t k", t=T) for d in dp_flat]
         dpt_codes = [keep.tile([P, T, 2, P], U32, name="dpt_codes%d" % g, align_bytes=64) for g in range(GROUPS)]
@@ -321,7 +322,7 @@ def tile_chebyshev_l3_sparsed32_stack_pb_v_kernel(
 
         def m_quantize(h):
             for a, n in ((0, N), (N, SPAN - N)):
-                col = W * h + a
+                col = SPAN * h + a
                 quantize(
                     m_codes[:, col : col + n],
                     m_scales[:, col : col + n],
@@ -338,16 +339,19 @@ def tile_chebyshev_l3_sparsed32_stack_pb_v_kernel(
 
         def product_0(g, t, w):
             ps = next_bank()
-            for h in range(2):
-                n = slice(SPAN * h + N * w, SPAN * h + N * (w + 1))
+            overlap = (N - P) * (1 - w)
+            for h, first, width, out in (
+                (w, (SPAN + P) * w, N, ps),
+                (1 - w, SPAN * (1 - w) + N * w, P, ps[:, overlap : overlap + P]),
+            ):
                 nc.tensor.matmul_mx(
-                    out=ps[:],
+                    out=out,
                     lhsT=dpt_codes[g][:, t, h, :].bitcast(E5M2),
                     lhsT_scale=dpt_scales[g][:, t, h, :],
-                    rhs=m_codes[:, n].bitcast(E4M3),
-                    rhs_scale=m_scales[:, n],
-                    start=(h == 0),
-                    stop=(h == 1),
+                    rhs=m_codes[:, first : first + width].bitcast(E4M3),
+                    rhs_scale=m_scales[:, first : first + width],
+                    start=(h == w),
+                    stop=(h != w),
                 )
             psum["o0", g, t, w] = ps
 
@@ -357,22 +361,23 @@ def tile_chebyshev_l3_sparsed32_stack_pb_v_kernel(
             copy(engine, sbuf["res0", g, t][:, N * w : N * (w + 1)], psum["o0", g, t, w][:])
 
         def window(i):
-            return (0, 0, 128, 128, 256, 384, 512, 512)[i]
+            return SHIFT * i // 64 * 64
 
         def pass_1(i, g, first=0):
             base = window(i)
             col = N * (i // 4) + 256 * (i % 2) + P * (i // 2 % 2)
             if g == first:
-                psum["o1", i] = next_bank()
-            nc.tensor.matmul_mx(
-                out=psum["o1", i],
-                lhsT=dpa_codes[g][:, col : col + P].bitcast(E5M2),
-                lhsT_scale=dpa_scales[g][:, col : col + P],
-                rhs=z_codes[g][:, base : base + N].bitcast(E4M3),
-                rhs_scale=z_scales[g][:, base : base + N],
-                start=(g == first),
-                stop=(g != first),
-            )
+                psum["o1", i] = next_bank(COVER)
+            for a, b in ((0, 256), (256, COVER)):
+                nc.tensor.matmul_mx(
+                    out=psum["o1", i][:, a:b],
+                    lhsT=dpa_codes[g][:, col : col + P].bitcast(E5M2),
+                    lhsT_scale=dpa_scales[g][:, col : col + P],
+                    rhs=z_codes[g][:, base + a : base + b].bitcast(E4M3),
+                    rhs_scale=z_scales[g][:, base + a : base + b],
+                    start=(g == first and a == 0),
+                    stop=(g != first and a > 0),
+                )
 
         def product_1(i):
             for g in range(GROUPS):
@@ -396,8 +401,6 @@ def tile_chebyshev_l3_sparsed32_stack_pb_v_kernel(
                         nc.vector.memset(rows[:, t, 0:first], 0.0)
                     if first + WIN1 < SPAN:
                         nc.vector.memset(rows[:, t, first + WIN1 : SPAN], 0.0)
-            nc.gpsimd.memset(m_codes[:, SPAN:W], 0)
-            nc.gpsimd.memset(m_scales[:, SPAN:W].bitcast(U32), 0)
             for n, (first, width) in enumerate(GAPS):
                 engine = nc.gpsimd if n == 0 else nc.vector
                 engine.memset(row1[:, first : first + width].bitcast(U32), 0)

@@ -83,6 +83,7 @@ def tile_chebyshev_l3_sparsed32_stack_pb_v_kernel(
         mask_few = keep.tile([P, WIN1], BF16, name="mask_few")
         picks = keep.tile([P, 16, 8], BF16, name="picks")
         ident = keep.tile([P, P], F32, name="ident")
+        ident_half = keep.tile([P, P], BF16, name="ident_half")
         row1 = keep.tile([P, ROW1], F32, name="row1")
 
         cw_il = keep.tile([P, 2, N, T], BF16, name="cw_il", align_bytes=64)
@@ -90,7 +91,8 @@ def tile_chebyshev_l3_sparsed32_stack_pb_v_kernel(
         cw_scales = keep.tile([P, 2, N], U8, name="cw_scales", align_bytes=64)
         g_codes = [keep.tile([P, T, P], U32, name="g_codes%d" % g, align_bytes=64) for g in range(GROUPS)]
         g_scales = [keep.tile([P, T, P], U8, name="g_scales%d" % g, align_bytes=64) for g in range(GROUPS)]
-        m_il = [keep.tile([P, SPAN, T], BF16, name="m_il%d" % h, align_bytes=64) for h in range(2)]
+        m_both = keep.tile([P, 2 * SPAN, T], BF16, name="m_both", align_bytes=64)
+        m_il = [m_both[:, SPAN * h : SPAN * (h + 1)] for h in range(2)]
         m_codes = keep.tile([P, 2 * SPAN], U32, name="m_codes", align_bytes=64)
         m_scales = keep.tile([P, 2 * SPAN], U8, name="m_scales", align_bytes=64)
         dp_flat = [keep.tile([P, T * K], BF16, name="dp%d" % g) for g in range(GROUPS)]
@@ -115,8 +117,9 @@ def tile_chebyshev_l3_sparsed32_stack_pb_v_kernel(
         psum = {}
         taken = []
 
-        def next_bank(width=N, dtype=F32):
-            taken.append(banks.tile([P, width], dtype, name="bank%d" % (len(taken) % 8)))
+        def next_bank(width=N, dtype=F32, bank=None):
+            bank = len(taken) % 8 if bank is None else bank
+            taken.append(banks.tile([P, width], dtype, name="bank%d" % bank))
             return taken[-1][:]
 
         sbuf = {}
@@ -168,6 +171,7 @@ def tile_chebyshev_l3_sparsed32_stack_pb_v_kernel(
 
         def prepare_mask():
             nc.vector.memset(mask_few[:], 0.0)
+            nc.vector.tensor_copy(out=ident_half[:], in_=ident[:])
             nc.vector.tensor_copy(out=picks[:], in_=ident[:, 0:8].unsqueeze(1).to_broadcast([P, 16, 8]))
 
         def spread_mask():
@@ -178,7 +182,7 @@ def tile_chebyshev_l3_sparsed32_stack_pb_v_kernel(
             psum["mask"] = ps
 
         def mask_copy():
-            nc.vector.tensor_copy(out=mask_o, in_=psum["mask"])
+            nc.scalar.copy(out=mask_o, in_=psum["mask"])
 
         def store_0(g, t):
             nc.sync.dma_start(out=out0_v[g, t], in_=sbuf["res0", g, t][:])
@@ -207,7 +211,7 @@ def tile_chebyshev_l3_sparsed32_stack_pb_v_kernel(
             psum["g", g, b] = ps
 
         def g_copy(g, b, engine="S"):
-            il = stage.tile([P, 2, P, 2], F32, name="words_il", align_bytes=64, bufs=6)
+            il = stage.tile([P, 2, P, 2], F32, name="words_il", align_bytes=64, bufs=2)
             copy(engine, il[:], psum["g", g, b][:].rearrange("p a u m -> p a m u"))
             sbuf["g", g, b] = il
 
@@ -262,34 +266,32 @@ def tile_chebyshev_l3_sparsed32_stack_pb_v_kernel(
             psum["dpt", g, t] = ps
 
         def dpt_copy(g, t, engine="S"):
-            if (g, t) == (0, HOLD):
-                il = keep.tile([P, 2, P, 2], F32, name="held", align_bytes=64)
-            else:
-                il = stage.tile([P, 2, P, 2], F32, name="words_il", align_bytes=64, bufs=6)
-            copy(engine, il[:], psum["dpt", g, t][:].rearrange("p h u m -> p h m u"))
-            sbuf["dpt", g, t] = il
+            if t % 2 == 0:
+                name = "held" if (g, t) == (0, HOLD) else "dpt_il%d%d" % (g, t)
+                sbuf["dpt", g, t // 2] = keep.tile([P, 2, 2, P, 2], F32, name=name, align_bytes=64)
+            copy(engine, sbuf["dpt", g, t // 2][:, t % 2], psum["dpt", g, t][:].rearrange("p h u m -> p h m u"))
 
-        def dpt_quantize(g, t):
+        def dpt_quantize(g, t0, t1):
             quantize(
-                dpt_codes[g][:, t].rearrange("p h m -> p (h m)"),
-                dpt_scales[g][:, t].rearrange("p h m -> p (h m)"),
-                sbuf["dpt", g, t][:].rearrange("p h m u -> p (h m u)").bitcast(BF16),
+                dpt_codes[g][:, t0:t1].rearrange("p t h m -> p (t h m)"),
+                dpt_scales[g][:, t0:t1].rearrange("p t h m -> p (t h m)"),
+                sbuf["dpt", g, t0 // 2][:, t0 % 2 : t0 % 2 + t1 - t0].rearrange("p t h m u -> p (t h m u)").bitcast(BF16),
                 E5M2,
             )
 
-        def dpa_copy(g, c, engine):
+        def dpa_copy(g, c, engine, m0=0, m1=P):
             src = dp[g][:, :, 256 * c : 256 * (c + 1)]
-            if (g, c) == (0, 2):
-                dpa_il[g, c] = keep.tile([P, 256, T], BF16, name="held", align_bytes=64)[:]
-            elif (g, c) == (0, 3):
-                dpa_il[g, c] = keep.tile([P, 256, T], BF16, name="dpa_il03", align_bytes=64)[:]
-            else:
-                if (g, c // 2) not in sbuf:
-                    sbuf[g, c // 2] = keep.tile([P, N, T], BF16, name="dpa_il%d%d" % (g, c // 2), align_bytes=64)
-                dpa_il[g, c] = sbuf[g, c // 2][:, 256 * (c % 2) : 256 * (c % 2 + 1), :]
+            if (g, c // 2) not in sbuf:
+                name = "held" if (g, c // 2) == (0, 1) else "dpa_il%d%d" % (g, c // 2)
+                sbuf[g, c // 2] = keep.tile([P, N, T], BF16, name=name, align_bytes=64)
+            dpa_il[g, c] = sbuf[g, c // 2][:, 256 * (c % 2) : 256 * (c % 2 + 1), :]
             dst = dpa_il[g, c]
             if engine == "G":
-                copy(engine, dst.rearrange("p (u m) t -> p u m t", u=2), src.rearrange("p t (m u) -> p u m t", u=2))
+                copy(
+                    engine,
+                    dst.rearrange("p (u m) t -> p u m t", u=2)[:, :, m0:m1],
+                    src.rearrange("p t (m u) -> p u m t", u=2)[:, :, m0:m1],
+                )
             else:
                 copy(
                     engine,
@@ -308,27 +310,49 @@ def tile_chebyshev_l3_sparsed32_stack_pb_v_kernel(
             else:
                 copy(engine, il.rearrange("p (c i) t -> p c t i", i=4), rows.rearrange("p t (c i) -> p c t i", i=4))
 
+        def weave(key, rows, u, bank):
+            ps = next_bank(2 * N, BF16, bank)
+            out = ps.rearrange("p (u m t) -> p t m u", u=u, t=T)
+            for n in range(2):
+                nc.tensor.matmul(
+                    out=out[:, :, P // u * n : P // u * (n + 1), :],
+                    lhsT=ident_half[:],
+                    rhs=rows[:, :, P * n : P * (n + 1)],
+                    start=True,
+                    stop=True,
+                )
+            psum[key] = ps
+
+        def z_weave(g, a, bank):
+            weave(("z", g, a), z_raw[g][:, :, a : a + 256], 1, bank)
+
+        def z_fetch(g, a):
+            nc.scalar.copy(out=z_il[g][:, a : a + 256, :].rearrange("p n t -> p (n t)"), in_=psum["z", g, a])
+
+        def dpa_weave(c, bank):
+            weave(("dpa", c), dp[1][:, :, 256 * c : 256 * (c + 1)], 2, bank)
+
+        def dpa_fetch(c):
+            if (1, 1) not in sbuf:
+                sbuf[1, 1] = keep.tile([P, N, T], BF16, name="dpa_il11", align_bytes=64)
+            dpa_il[1, c] = sbuf[1, 1][:, 256 * (c % 2) : 256 * (c % 2 + 1), :]
+            nc.scalar.copy(out=dpa_il[1, c].rearrange("p n t -> p (n t)"), in_=psum["dpa", c])
+
         def m_multiply(h):
             for l in range(2):
                 nc.vector.tensor_tensor(
                     out=t3_windows(h, l),
                     in0=t3_windows(h, l),
-                    in1=mask_o.unsqueeze(1).to_broadcast([P, 2, WIN1]),
+                    in1=psum["mask"].unsqueeze(1).to_broadcast([P, 2, WIN1]),
                     op=MULT,
                 )
 
         def m_copy(h, a, b, engine):
             interleave(engine, m_il[h][:, a:b, :], t3_rows(h)[:, :, a:b])
 
-        def m_quantize(h):
-            for a, n in ((0, N), (N, SPAN - N)):
-                col = SPAN * h + a
-                quantize(
-                    m_codes[:, col : col + n],
-                    m_scales[:, col : col + n],
-                    m_il[h][:, a : a + n, :].rearrange("p n t -> p (n t)"),
-                    E4M3,
-                )
+        def m_quantize():
+            for n in (slice(0, W), slice(W, 2 * SPAN)):
+                quantize(m_codes[:, n], m_scales[:, n], m_both[:, n].rearrange("p n t -> p (n t)"), E4M3)
 
         def z_copy(g, a, b, engine):
             interleave(engine, z_il[g][:, a:b, :], z_raw[g][:, :, a:b])
@@ -337,8 +361,8 @@ def tile_chebyshev_l3_sparsed32_stack_pb_v_kernel(
             n = slice(a, b)
             quantize(z_codes[g][:, n], z_scales[g][:, n], z_il[g][:, n, :].rearrange("p n t -> p (n t)"), E4M3)
 
-        def product_0(g, t, w):
-            ps = next_bank()
+        def product_0(g, t, w, bank):
+            ps = next_bank(N, F32, bank)
             overlap = (N - P) * (1 - w)
             for h, first, width, out in (
                 (w, (SPAN + P) * w, N, ps),
@@ -363,11 +387,11 @@ def tile_chebyshev_l3_sparsed32_stack_pb_v_kernel(
         def window(i):
             return SHIFT * i // 64 * 64
 
-        def pass_1(i, g, first=0):
+        def pass_1(i, g, first=0, bank=None):
             base = window(i)
             col = N * (i // 4) + 256 * (i % 2) + P * (i // 2 % 2)
             if g == first:
-                psum["o1", i] = next_bank(COVER)
+                psum["o1", i] = next_bank(COVER, F32, bank)
             for a, b in ((0, 256), (256, COVER)):
                 nc.tensor.matmul_mx(
                     out=psum["o1", i][:, a:b],
@@ -379,9 +403,9 @@ def tile_chebyshev_l3_sparsed32_stack_pb_v_kernel(
                     stop=(g != first and a > 0),
                 )
 
-        def product_1(i):
+        def product_1(i, bank):
             for g in range(GROUPS):
-                pass_1(i, g)
+                pass_1(i, g, 0, bank)
 
         def result_1(i):
             first = SHIFT * i - window(i)
@@ -419,9 +443,9 @@ def tile_chebyshev_l3_sparsed32_stack_pb_v_kernel(
                 g_transpose(g, b)
                 g_copy(g, b)
 
-            def products_0(g, t):
+            def products_0(g, t, pair=(None, None)):
                 for w in range(2):
-                    product_0(g, t, w)
+                    product_0(g, t, w, pair[w])
 
             def results_0(g, t, engines="SS"):
                 for w in range(2):
@@ -447,7 +471,7 @@ def tile_chebyshev_l3_sparsed32_stack_pb_v_kernel(
             load_z(0)
             load_x2_second()
             load_z(1)
-            for i in FILL[:5]:
+            for i in FILL[:6]:
                 zero_1(i)
 
             cw_copy(0, 0, 0, 16, "V")
@@ -455,11 +479,11 @@ def tile_chebyshev_l3_sparsed32_stack_pb_v_kernel(
             cw_copy(0, 1, 5, 16, "S")
             g_turn(0, 0)
             spread_mask()
-            cw_copy(1, 0, 0, 8, "V")
-            mask_copy()
+            cw_copy(1, 0, 0, 12, "V")
             cw_quantize(0)
             g_quantize(0, 0)
-            cw_copy(1, 0, 8, 16, "S")
+            mask_copy()
+            cw_copy(1, 0, 12, 16, "S")
             g_turn(0, 1)
             cw_copy(1, 1, 0, 16, "S")
             m_multiply(0)
@@ -485,78 +509,87 @@ def tile_chebyshev_l3_sparsed32_stack_pb_v_kernel(
                 turn(0, t)
 
             g_quantize(1, 0)
-            m_quantize(0)
-            m_quantize(1)
-            dpt_quantize(0, 0)
+            m_quantize()
             g_quantize(1, 1)
-            for t in range(1, T):
-                dpt_quantize(0, t)
-            for c in (2, 3, 1):
+            dpt_quantize(0, 0, 1)
+            dpt_quantize(0, 1, 2)
+            dpt_quantize(0, 2, 4)
+            for c in (2, 3):
                 dpa_copy(0, c, "G")
+            dpa_copy(0, 1, "G")
             for t in range(2):
                 for h in range(2):
                     dx3(1, t, h)
             z_copy(0, 0, 512, "S")
             products_0(0, 0)
             results_0(0, 0)
-            for i in FILL[5:7]:
-                zero_1(i)
             for t in range(2):
                 for h in range(2):
                     dp3(1, t, h)
-            for t in range(2, 4):
-                for h in range(2):
-                    dx3(1, t, h)
-            z_copy(0, 512, 768, "S")
-            turn(1, 0)
-            turn(1, 1)
+            for h in range(2):
+                dx3(1, 2, h)
             products_0(0, 1)
             results_0(0, 1)
-            zero_1(FILL[7])
+            zero_1(FILL[6])
+            for h in range(2):
+                dx3(1, 3, h)
+            turn(1, 0)
+            turn(1, 1)
             for t in range(2, 4):
                 for h in range(2):
                     dp3(1, t, h)
-            turn(1, 2)
-            turn(1, 3)
             products_0(0, 2)
             results_0(0, 2)
+            zero_1(FILL[7])
+            turn(1, 2)
+            turn(1, 3)
             z_copy(1, 0, 512, "V")
-            dpt_quantize(1, 0)
-            dpt_quantize(1, 1)
+            dpt_quantize(1, 0, 2)
             z_quantize(0, 0, 512)
             for c in range(2):
                 dpa_copy(1, c, "V")
-            dpt_quantize(1, 2)
-            dpt_quantize(1, 3)
+            dpt_quantize(1, 2, 4)
             products_0(0, 3)
             results_0(0, 3)
             z_quantize(1, 0, 512)
             dpa_quantize(0, 0, 2)
-            z_copy(1, 512, 1024, "V")
             dpa_quantize(1, 0, 2)
+            z_copy(1, 512, 1024, "V")
+            z_weave(0, 512, 5)
+            products_0(1, 0, (6, 7))
+            results_0(1, 0)
+            products_0(1, 1, (0, 1))
+            results_0(1, 1)
+            z_fetch(0, 512)
+            dpa_weave(2, 2)
+            products_0(1, 2, (3, 4))
+            results_0(1, 2)
+            dpa_fetch(2)
+            dpa_weave(3, 6)
+            products_0(1, 3, (7, 0))
+            results_0(1, 3)
+            dpa_fetch(3)
+            product_1(0, 1)
+            product_1(1, 5)
+            z_weave(0, 768, 3)
+            z_fetch(0, 768)
             z_quantize(0, 512, 768)
             z_quantize(1, 512, 1024)
-            for t in range(T):
-                products_0(1, t)
-                results_0(1, t)
-            dpa_copy(1, 3, "S")
-            z_copy(0, 768, 1024, "S")
-            dpa_copy(1, 2, "V")
-            for i in range(4):
-                product_1(i)
-            dpa_quantize(0, 2, 3)
-            dpa_quantize(0, 3, 4)
-            dpa_quantize(1, 2, 3)
-            product_1(4)
-            pass_1(6, 1, first=1)
             finish_1(0)
             finish_1(1)
-            dpa_quantize(1, 3, 4)
-            for i in (5, 7):
-                pass_1(i, 1, first=1)
+            product_1(2, 4)
+            product_1(3, 2)
+            dpa_quantize(0, 2, 4)
+            dpa_quantize(1, 2, 3)
+            product_1(4, 7)
+            pass_1(6, 1, 1, 0)
             finish_1(2)
             z_quantize(0, 768, 1024)
-            for i in range(5, 8):
-                pass_1(i, 0, first=1)
-            for i in range(3, 8):
+            dpa_quantize(1, 3, 4)
+            pass_1(6, 0, 1)
+            pass_1(5, 0, 0, 1)
+            pass_1(7, 0, 0, 5)
+            pass_1(5, 1)
+            pass_1(7, 1)
+            for i in (3, 4, 6, 5, 7):
                 finish_1(i)

@@ -295,8 +295,8 @@ def tile_chebyshev_l3_sparsed32_stack_pb_v_kernel(
             else:
                 copy(
                     engine,
-                    dst.rearrange("p (u m i) t -> p u m t i", u=2, i=4),
-                    src.rearrange("p t (m i u) -> p u m t i", u=2, i=4),
+                    dst.rearrange("p (u m i) t -> p u m t i", u=2, i=4)[:, :, m0 // 4 : m1 // 4],
+                    src.rearrange("p t (m i u) -> p u m t i", u=2, i=4)[:, :, m0 // 4 : m1 // 4],
                 )
 
         def dpa_quantize(g, c0, c1):
@@ -327,7 +327,8 @@ def tile_chebyshev_l3_sparsed32_stack_pb_v_kernel(
             weave(("z", g, a), z_raw[g][:, :, a : a + 256], 1, bank)
 
         def z_fetch(g, a):
-            nc.scalar.copy(out=z_il[g][:, a : a + 256, :].rearrange("p n t -> p (n t)"), in_=psum["z", g, a])
+            out = z_il[g][:, a : a + 256, :].rearrange("p n t -> p (n t)")
+            nc.scalar.copy(out=out.bitcast(F32), in_=psum["z", g, a].bitcast(F32))
 
         def dpa_weave(c, bank):
             weave(("dpa", c), dp[1][:, :, 256 * c : 256 * (c + 1)], 2, bank)
@@ -336,7 +337,8 @@ def tile_chebyshev_l3_sparsed32_stack_pb_v_kernel(
             if (1, 1) not in sbuf:
                 sbuf[1, 1] = keep.tile([P, N, T], BF16, name="dpa_il11", align_bytes=64)
             dpa_il[1, c] = sbuf[1, 1][:, 256 * (c % 2) : 256 * (c % 2 + 1), :]
-            nc.scalar.copy(out=dpa_il[1, c].rearrange("p n t -> p (n t)"), in_=psum["dpa", c])
+            out = dpa_il[1, c].rearrange("p n t -> p (n t)")
+            nc.scalar.copy(out=out.bitcast(F32), in_=psum["dpa", c].bitcast(F32))
 
         def m_multiply(h):
             for l in range(2):
@@ -516,7 +518,7 @@ def tile_chebyshev_l3_sparsed32_stack_pb_v_kernel(
             dpt_quantize(0, 2, 4)
             for c in (2, 3):
                 dpa_copy(0, c, "G")
-            dpa_copy(0, 1, "G")
+            dpa_copy(0, 1, "G", 0, 64)
             for t in range(2):
                 for h in range(2):
                     dx3(1, t, h)
@@ -530,6 +532,7 @@ def tile_chebyshev_l3_sparsed32_stack_pb_v_kernel(
                 dx3(1, 2, h)
             products_0(0, 1)
             results_0(0, 1)
+            z_copy(0, 512, 768, "S")
             zero_1(FILL[6])
             for h in range(2):
                 dx3(1, 3, h)
@@ -543,6 +546,7 @@ def tile_chebyshev_l3_sparsed32_stack_pb_v_kernel(
             zero_1(FILL[7])
             turn(1, 2)
             turn(1, 3)
+            dpa_copy(0, 1, "V", 64, P)
             z_copy(1, 0, 512, "V")
             dpt_quantize(1, 0, 2)
             z_quantize(0, 0, 512)
@@ -555,41 +559,35 @@ def tile_chebyshev_l3_sparsed32_stack_pb_v_kernel(
             dpa_quantize(0, 0, 2)
             dpa_quantize(1, 0, 2)
             z_copy(1, 512, 1024, "V")
-            z_weave(0, 512, 5)
+            dpa_weave(2, 5)
             products_0(1, 0, (6, 7))
             results_0(1, 0)
             products_0(1, 1, (0, 1))
             results_0(1, 1)
-            z_fetch(0, 512)
-            dpa_weave(2, 2)
+            dpa_weave(3, 2)
             products_0(1, 2, (3, 4))
             results_0(1, 2)
-            dpa_fetch(2)
-            dpa_weave(3, 6)
-            products_0(1, 3, (7, 0))
+            products_0(1, 3, (6, 7))
             results_0(1, 3)
-            dpa_fetch(3)
-            product_1(0, 1)
-            product_1(1, 5)
+            product_1(0, 0)
+            product_1(1, 1)
             z_weave(0, 768, 3)
+            dpa_fetch(2)
+            dpa_fetch(3)
             z_fetch(0, 768)
             z_quantize(0, 512, 768)
             z_quantize(1, 512, 1024)
+            product_1(2, 4)
+            product_1(3, 6)
             finish_1(0)
             finish_1(1)
-            product_1(2, 4)
-            product_1(3, 2)
             dpa_quantize(0, 2, 4)
-            dpa_quantize(1, 2, 3)
-            product_1(4, 7)
-            pass_1(6, 1, 1, 0)
             finish_1(2)
+            dpa_quantize(1, 2, 4)
+            product_1(4, 7)
             z_quantize(0, 768, 1024)
-            dpa_quantize(1, 3, 4)
-            pass_1(6, 0, 1)
-            pass_1(5, 0, 0, 1)
-            pass_1(7, 0, 0, 5)
-            pass_1(5, 1)
-            pass_1(7, 1)
-            for i in (3, 4, 6, 5, 7):
+            product_1(5, 0)
+            product_1(6, 1)
+            product_1(7, 5)
+            for i in range(3, 8):
                 finish_1(i)

@@ -26,7 +26,7 @@ HOLD = 2
 L_STEP = 2 * SPAN + SHIFT
 U_STEP = SPAN + 2 * SHIFT
 FILL = (0, 7, 1, 6, 2, 5, 3, 4)
-NARROW = (3, 4, 5, 6)
+NARROW = (1, 2, 3, 4, 5, 6)
 
 
 def stored_zeros(i):
@@ -195,12 +195,15 @@ def tile_chebyshev_l3_sparsed32_stack_pb_v_kernel(
                 in_=row1[:, PLACE[i] - left : PLACE[i] + WIN1 + right],
             )
 
+        def zeros(width):
+            return row1[32:96, WIN1 : WIN1 + width].unsqueeze(1).to_broadcast([64, 2, width])
+
         def zero_1(i):
             left, right = SHIFT * i, W - WIN1 - SHIFT * i
             if left > right or i in NARROW:
-                nc.sync.dma_start(out=out1_v[i, :, :, 0:left], in_=row1[:, WIN1 : WIN1 + left])
+                nc.sync.dma_start(out=out1_v[i, :, :, 0:left], in_=zeros(left))
             if left < right or i in NARROW:
-                nc.sync.dma_start(out=out1_v[i, :, :, left + WIN1 : W], in_=row1[:, WIN1 : WIN1 + right])
+                nc.sync.dma_start(out=out1_v[i, :, :, left + WIN1 : W], in_=zeros(right))
 
         def g_transpose(g, b):
             ps = next_bank().rearrange("p (a u m) -> p a u m", a=2, u=2)
@@ -427,9 +430,10 @@ def tile_chebyshev_l3_sparsed32_stack_pb_v_kernel(
                         nc.vector.memset(rows[:, t, 0:first], 0.0)
                     if first + WIN1 < SPAN:
                         nc.vector.memset(rows[:, t, first + WIN1 : SPAN], 0.0)
-            for n, (first, width) in enumerate(GAPS):
-                engine = nc.gpsimd if n == 0 else nc.vector
-                engine.memset(row1[:, first : first + width].bitcast(U32), 0)
+            for part in (32, 64):
+                nc.gpsimd.memset(row1[part : part + 32, WIN1:W].bitcast(U32), 0)
+            for first, width in GAPS[1:]:
+                nc.vector.memset(row1[:, first : first + width].bitcast(U32), 0)
 
         with tc.manual_schedule():
 

@@ -26,34 +26,7 @@ HOLD = 2
 L_STEP = 2 * SPAN + SHIFT
 U_STEP = SPAN + 2 * SHIFT
 FILL = (0, 7, 1, 6, 2, 5, 3, 4)
-NARROW = (1, 2, 3, 4, 5, 6)
 
-
-def stored_zeros(i):
-    left, right = SHIFT * i, W - WIN1 - SHIFT * i
-    if i in NARROW:
-        return 0, 0
-    return (left, 0) if left < right else (0, right)
-
-
-def lay_out_row1():
-    order = [i for k in range(4) for i in (k, 7 - k)]
-    place, gaps, col = {}, [], 0
-    for n, i in enumerate(order):
-        place[i] = col
-        col = col + WIN1
-        gap = stored_zeros(i)[1]
-        if n + 1 < len(order):
-            gap = max(gap, stored_zeros(order[n + 1])[0])
-        if n == 0:
-            gap = W - WIN1
-        if gap > 0:
-            gaps.append((col, gap))
-        col = col + gap
-    return place, gaps, col
-
-
-PLACE, GAPS, ROW1 = lay_out_row1()
 
 FLOPS = 2 * (B * O * K + 2 * B * K * W)
 BYTES = 2 * (4 * 1024 * 1024 + 2 * 512 * 1024) + 4 * 2 * 1024 * 1024
@@ -79,12 +52,12 @@ def tile_chebyshev_l3_sparsed32_stack_pb_v_kernel(
         z_raw = [keep.tile([P, T, W], BF16, name="z_raw%d" % g) for g in range(GROUPS)]
         t3_raw = [keep.tile([P, L_STEP + 2 * U_STEP], BF16, name="t3_raw%d" % h) for h in range(2)]
         mask_row = keep.tile([P, WIN1], BF16, name="mask_row")
-        mask_o = mask_row[:]
         mask_few = keep.tile([P, WIN1], BF16, name="mask_few")
         picks = keep.tile([P, 16, 8], BF16, name="picks")
         ident = keep.tile([P, P], F32, name="ident")
         ident_half = keep.tile([P, P], BF16, name="ident_half")
-        row1 = keep.tile([P, ROW1], F32, name="row1")
+        row1 = keep.tile([P, 8, WIN1], F32, name="row1")
+        zero_row = keep.tile([P, W - WIN1], F32, name="zero_row")
 
         cw_il = keep.tile([P, 2, N, T], BF16, name="cw_il", align_bytes=64)
         cw_codes = keep.tile([P, 2, N], U32, name="cw_codes", align_bytes=64)
@@ -99,7 +72,6 @@ def tile_chebyshev_l3_sparsed32_stack_pb_v_kernel(
         dp = [d[:].rearrange("p (t k) -> p t k", t=T) for d in dp_flat]
         dpt_codes = [keep.tile([P, T, 2, P], U32, name="dpt_codes%d" % g, align_bytes=64) for g in range(GROUPS)]
         dpt_scales = [keep.tile([P, T, 2, P], U8, name="dpt_scales%d" % g, align_bytes=64) for g in range(GROUPS)]
-        dpa_il = {}
         dpa_codes = [keep.tile([P, K], U32, name="dpa_codes%d" % g, align_bytes=64) for g in range(GROUPS)]
         dpa_scales = [keep.tile([P, K], U8, name="dpa_scales%d" % g, align_bytes=64) for g in range(GROUPS)]
         z_il = [keep.tile([P, W, T], BF16, name="z_il%d" % g, align_bytes=64) for g in range(GROUPS)]
@@ -116,9 +88,12 @@ def tile_chebyshev_l3_sparsed32_stack_pb_v_kernel(
 
         psum = {}
         taken = []
+        in_turn = []
 
         def next_bank(width=N, dtype=F32, bank=None):
-            bank = len(taken) % 8 if bank is None else bank
+            if bank is None:
+                bank = len(in_turn) % 8
+                in_turn.append(bank)
             taken.append(banks.tile([P, width], dtype, name="bank%d" % bank))
             return taken[-1][:]
 
@@ -175,35 +150,26 @@ def tile_chebyshev_l3_sparsed32_stack_pb_v_kernel(
             nc.vector.tensor_copy(out=picks[:], in_=ident[:, 0:8].unsqueeze(1).to_broadcast([P, 16, 8]))
 
         def spread_mask():
-            ps = next_bank(WIN1, BF16)
+            psum["mask"] = next_bank(WIN1, BF16)
             nc.tensor.matmul(
-                out=ps, lhsT=picks[:].rearrange("p s j -> p (s j)"), rhs=mask_few[:], start=True, stop=True
+                out=psum["mask"], lhsT=picks[:].rearrange("p s j -> p (s j)"), rhs=mask_few[:], start=True, stop=True
             )
-            psum["mask"] = ps
 
         def mask_copy():
-            nc.scalar.copy(out=mask_o, in_=psum["mask"])
+            nc.scalar.copy(out=mask_row[:], in_=psum["mask"])
 
         def store_0(g, t):
             nc.sync.dma_start(out=out0_v[g, t], in_=sbuf["res0", g, t][:])
 
         def store_1(i):
-            left, right = stored_zeros(i)
-            first = SHIFT * i
-            nc.sync.dma_start(
-                out=out1_v[i, :, :, first - left : first + WIN1 + right],
-                in_=row1[:, PLACE[i] - left : PLACE[i] + WIN1 + right],
-            )
-
-        def zeros(width):
-            return row1[32:96, WIN1 : WIN1 + width].unsqueeze(1).to_broadcast([64, 2, width])
+            cols = slice(SHIFT * i, SHIFT * i + WIN1)
+            nc.sync.dma_start(out=out1_v[i, :, :, cols], in_=row1[:, i])
 
         def zero_1(i):
-            left, right = SHIFT * i, W - WIN1 - SHIFT * i
-            if left > right or i in NARROW:
-                nc.sync.dma_start(out=out1_v[i, :, :, 0:left], in_=zeros(left))
-            if left < right or i in NARROW:
-                nc.sync.dma_start(out=out1_v[i, :, :, left + WIN1 : W], in_=zeros(right))
+            for first, last in ((0, SHIFT * i), (SHIFT * i + WIN1, W)):
+                if last > first:
+                    source = zero_row[32:96, 0 : last - first].unsqueeze(1).to_broadcast([64, 2, last - first])
+                    nc.sync.dma_start(out=out1_v[i, :, :, first:last], in_=source)
 
         def g_transpose(g, b):
             ps = next_bank().rearrange("p (a u m) -> p a u m", a=2, u=2)
@@ -282,13 +248,15 @@ def tile_chebyshev_l3_sparsed32_stack_pb_v_kernel(
                 E5M2,
             )
 
-        def dpa_copy(g, c, engine, m0=0, m1=P):
-            src = dp[g][:, :, 256 * c : 256 * (c + 1)]
+        def dpa_piece(g, c):
             if (g, c // 2) not in sbuf:
                 name = "held" if (g, c // 2) == (0, 1) else "dpa_il%d%d" % (g, c // 2)
                 sbuf[g, c // 2] = keep.tile([P, N, T], BF16, name=name, align_bytes=64)
-            dpa_il[g, c] = sbuf[g, c // 2][:, 256 * (c % 2) : 256 * (c % 2 + 1), :]
-            dst = dpa_il[g, c]
+            return sbuf[g, c // 2][:, 256 * (c % 2) : 256 * (c % 2 + 1), :]
+
+        def dpa_copy(g, c, engine, m0=0, m1=P):
+            src = dp[g][:, :, 256 * c : 256 * (c + 1)]
+            dst = dpa_piece(g, c)
             if engine == "G":
                 copy(
                     engine,
@@ -304,7 +272,7 @@ def tile_chebyshev_l3_sparsed32_stack_pb_v_kernel(
 
         def dpa_quantize(g, c0, c1):
             n = slice(256 * c0, 256 * c1)
-            values = dpa_il[g, c0] if c1 == c0 + 1 else sbuf[g, c0 // 2][:]
+            values = dpa_piece(g, c0) if c1 == c0 + 1 else sbuf[g, c0 // 2][:]
             quantize(dpa_codes[g][:, n], dpa_scales[g][:, n], values.rearrange("p n t -> p (n t)"), E5M2)
 
         def interleave(engine, il, rows):
@@ -313,35 +281,17 @@ def tile_chebyshev_l3_sparsed32_stack_pb_v_kernel(
             else:
                 copy(engine, il.rearrange("p (c i) t -> p c t i", i=4), rows.rearrange("p t (c i) -> p c t i", i=4))
 
-        def weave(key, rows, u, bank):
+        def dpa_weave(g, c, bank):
             ps = next_bank(2 * N, BF16, bank)
-            out = ps.rearrange("p (u m t) -> p t m u", u=u, t=T)
-            for n in range(2):
-                nc.tensor.matmul(
-                    out=out[:, :, P // u * n : P // u * (n + 1), :],
-                    lhsT=ident_half[:],
-                    rhs=rows[:, :, P * n : P * (n + 1)],
-                    start=True,
-                    stop=True,
-                )
-            psum[key] = ps
+            out = ps.rearrange("p (u a m t) -> p a t m u", u=2, a=2, t=T)
+            rows = dp[g][:, :, 256 * c : 256 * (c + 1)].rearrange("p t (a e) -> p a t e", a=2)
+            for a in range(2):
+                nc.tensor.matmul(out=out[:, a], lhsT=ident_half[:], rhs=rows[:, a], start=True, stop=True)
+            psum["dpa", g, c] = ps
 
-        def z_weave(g, a, bank):
-            weave(("z", g, a), z_raw[g][:, :, a : a + 256], 1, bank)
-
-        def z_fetch(g, a):
-            out = z_il[g][:, a : a + 256, :].rearrange("p n t -> p (n t)")
-            nc.scalar.copy(out=out.bitcast(F32), in_=psum["z", g, a].bitcast(F32))
-
-        def dpa_weave(c, bank):
-            weave(("dpa", c), dp[1][:, :, 256 * c : 256 * (c + 1)], 2, bank)
-
-        def dpa_fetch(c):
-            if (1, 1) not in sbuf:
-                sbuf[1, 1] = keep.tile([P, N, T], BF16, name="dpa_il11", align_bytes=64)
-            dpa_il[1, c] = sbuf[1, 1][:, 256 * (c % 2) : 256 * (c % 2 + 1), :]
-            out = dpa_il[1, c].rearrange("p n t -> p (n t)")
-            nc.scalar.copy(out=out.bitcast(F32), in_=psum["dpa", c].bitcast(F32))
+        def dpa_fetch(g, c):
+            out = dpa_piece(g, c).rearrange("p n t -> p (n t)")
+            nc.scalar.copy(out=out.bitcast(F32), in_=psum["dpa", g, c].bitcast(F32))
 
         def m_multiply(h):
             for l in range(2):
@@ -415,9 +365,9 @@ def tile_chebyshev_l3_sparsed32_stack_pb_v_kernel(
         def result_1(i):
             first = SHIFT * i - window(i)
             nc.vector.tensor_tensor(
-                out=row1[:, PLACE[i] : PLACE[i] + WIN1],
+                out=row1[:, i],
                 in0=psum["o1", i][:, first : first + WIN1],
-                in1=mask_o,
+                in1=mask_row[:],
                 op=MULT,
             )
 
@@ -431,9 +381,7 @@ def tile_chebyshev_l3_sparsed32_stack_pb_v_kernel(
                     if first + WIN1 < SPAN:
                         nc.vector.memset(rows[:, t, first + WIN1 : SPAN], 0.0)
             for part in (32, 64):
-                nc.gpsimd.memset(row1[part : part + 32, WIN1:W].bitcast(U32), 0)
-            for first, width in GAPS[1:]:
-                nc.vector.memset(row1[:, first : first + width].bitcast(U32), 0)
+                nc.gpsimd.memset(zero_row[part : part + 32, :].bitcast(U32), 0)
 
         with tc.manual_schedule():
 
@@ -500,8 +448,8 @@ def tile_chebyshev_l3_sparsed32_stack_pb_v_kernel(
             dx_dp(0, 1, 0)
             cw_quantize(1)
             m_multiply(1)
-            m_copy(1, 0, 256, "G")
-            m_copy(1, 256, SPAN, "S")
+            m_copy(1, 0, 208, "G")
+            m_copy(1, 208, SPAN, "S")
             dx_dp(0, 2, 0)
             dx_dp(0, 3, 0)
             dpa_copy(0, 0, "G")
@@ -520,9 +468,9 @@ def tile_chebyshev_l3_sparsed32_stack_pb_v_kernel(
             dpt_quantize(0, 0, 1)
             dpt_quantize(0, 1, 2)
             dpt_quantize(0, 2, 4)
-            for c in (2, 3):
-                dpa_copy(0, c, "G")
-            dpa_copy(0, 1, "G", 0, 64)
+            dpa_copy(0, 2, "G")
+            z_copy(0, 768, 1024, "G")
+            dpa_copy(0, 1, "G", 0, 48)
             for t in range(2):
                 for h in range(2):
                     dx3(1, t, h)
@@ -550,7 +498,7 @@ def tile_chebyshev_l3_sparsed32_stack_pb_v_kernel(
             zero_1(FILL[7])
             turn(1, 2)
             turn(1, 3)
-            dpa_copy(0, 1, "V", 64, P)
+            dpa_copy(0, 1, "V", 48, P)
             z_copy(1, 0, 512, "V")
             dpt_quantize(1, 0, 2)
             z_quantize(0, 0, 512)
@@ -563,35 +511,36 @@ def tile_chebyshev_l3_sparsed32_stack_pb_v_kernel(
             dpa_quantize(0, 0, 2)
             dpa_quantize(1, 0, 2)
             z_copy(1, 512, 1024, "V")
-            dpa_weave(2, 5)
+            dpa_weave(1, 2, 5)
             products_0(1, 0, (6, 7))
             results_0(1, 0)
             products_0(1, 1, (0, 1))
             results_0(1, 1)
-            dpa_weave(3, 2)
+            dpa_weave(0, 3, 2)
             products_0(1, 2, (3, 4))
             results_0(1, 2)
             products_0(1, 3, (6, 7))
             results_0(1, 3)
             product_1(0, 0)
             product_1(1, 1)
-            z_weave(0, 768, 3)
-            dpa_fetch(2)
-            dpa_fetch(3)
-            z_fetch(0, 768)
-            z_quantize(0, 512, 768)
+            dpa_weave(1, 3, 3)
+            dpa_fetch(1, 2)
+            dpa_fetch(0, 3)
+            dpa_fetch(1, 3)
+            z_quantize(0, 512, 1024)
             z_quantize(1, 512, 1024)
             product_1(2, 4)
             product_1(3, 6)
             finish_1(0)
             finish_1(1)
-            dpa_quantize(0, 2, 4)
-            finish_1(2)
-            dpa_quantize(1, 2, 4)
+            dpa_quantize(0, 2, 3)
+            dpa_quantize(1, 2, 3)
             product_1(4, 7)
-            z_quantize(0, 768, 1024)
-            product_1(5, 0)
-            product_1(6, 1)
+            product_1(6, 0)
+            finish_1(2)
+            dpa_quantize(0, 3, 4)
+            dpa_quantize(1, 3, 4)
+            product_1(5, 1)
             product_1(7, 5)
-            for i in range(3, 8):
+            for i in (3, 4, 6, 5, 7):
                 finish_1(i)

from contextlib import ExitStack

import concourse.mybir as mybir
from concourse.masks import make_identity

F32 = mybir.dt.float32
BF16 = mybir.dt.bfloat16
U32 = mybir.dt.uint32
U8 = mybir.dt.uint8
E4M3 = mybir.dt.float8_e4m3fn_x4
E5M2 = mybir.dt.float8_e5m2_x4
MULT = mybir.AluOpType.mult
ADD = mybir.AluOpType.add
COPY = mybir.ActivationFunctionType.Copy

P = 128
B, O, K, W = 1024, 512, 1024, 1024
GROUPS = 2
T = 4
N = 512
SPAN = 640
WIN1 = 352
SHIFT = 96
COVER = 384
HOLD = 2
L_STEP = 2 * SPAN + SHIFT
U_STEP = SPAN + 2 * SHIFT
FILL = (0, 7, 1, 6, 2, 5, 3, 4)


FLOPS = 2 * (B * O * K + 2 * B * K * W)
BYTES = 2 * (4 * 1024 * 1024 + 2 * 512 * 1024) + 4 * 2 * 1024 * 1024


def tile_chebyshev_l3_sparsed32_stack_pb_v_kernel(
    tc, z, T3, mask, x1, x2, C_w, C_b, p3, grad_out, out_0, out_1
):
    nc = tc.nc
    with ExitStack() as ctx:
        keep = ctx.enter_context(tc.tile_pool(name="keep", bufs=1))
        stage = ctx.enter_context(tc.tile_pool(name="stage", bufs=4))
        stage0 = ctx.enter_context(tc.tile_pool(name="stage0", bufs=8))
        banks = ctx.enter_context(tc.psum_pool(name="banks", bufs=1))

        cw_raw = keep.tile([P, T, K], BF16, name="cw_raw")
        g_first = [keep.tile([P, 2, O], BF16, name="g_first%d" % b) for b in range(2)]
        g_second = keep.tile([P, T, O], BF16, name="g_second")
        g_raw = [[g_first[b][:] for b in range(2)], [g_second[:, 2 * b : 2 * b + 2] for b in range(2)]]
        x2_first = [keep.tile([P, 2, K], BF16, name="x2_first%d" % b) for b in range(2)]
        x2_second = keep.tile([P, T, K], BF16, name="x2_second")
        x2_raw = [[x2_first[b][:] for b in range(2)], [x2_second[:, 2 * b : 2 * b + 2] for b in range(2)]]
        z_raw = [keep.tile([P, T, W], BF16, name="z_raw%d" % g) for g in range(GROUPS)]
        t3_raw = [keep.tile([P, L_STEP + 2 * U_STEP], BF16, name="t3_raw%d" % h) for h in range(2)]
        mask_row = keep.tile([P, WIN1], BF16, name="mask_row")
        mask_few = keep.tile([P, WIN1], BF16, name="mask_few")
        picks = keep.tile([P, 16, 8], BF16, name="picks")
        ident = keep.tile([P, P], F32, name="ident")
        ident_half = keep.tile([P, P], BF16, name="ident_half")
        row1 = keep.tile([P, 8, WIN1], F32, name="row1")
        zero_row = keep.tile([P, W - WIN1], F32, name="zero_row")

        cw_il = keep.tile([P, 2, N, T], BF16, name="cw_il", align_bytes=64)
        cw_codes = keep.tile([P, 2, N], U32, name="cw_codes", align_bytes=64)
        cw_scales = keep.tile([P, 2, N], U8, name="cw_scales", align_bytes=64)
        g_codes = [keep.tile([P, T, P], U32, name="g_codes%d" % g, align_bytes=64) for g in range(GROUPS)]
        g_scales = [keep.tile([P, T, P], U8, name="g_scales%d" % g, align_bytes=64) for g in range(GROUPS)]
        m_both = keep.tile([P, 2 * SPAN, T], BF16, name="m_both", align_bytes=64)
        m_il = [m_both[:, SPAN * h : SPAN * (h + 1)] for h in range(2)]
        m_codes = keep.tile([P, 2 * SPAN], U32, name="m_codes", align_bytes=64)
        m_scales = keep.tile([P, 2 * SPAN], U8, name="m_scales", align_bytes=64)
        dp_flat = [keep.tile([P, T * K], BF16, name="dp%d" % g) for g in range(GROUPS)]
        dp = [d[:].rearrange("p (t k) -> p t k", t=T) for d in dp_flat]
        dpt_codes = [keep.tile([P, T, 2, P], U32, name="dpt_codes%d" % g, align_bytes=64) for g in range(GROUPS)]
        dpt_scales = [keep.tile([P, T, 2, P], U8, name="dpt_scales%d" % g, align_bytes=64) for g in range(GROUPS)]
        dpa_codes = [keep.tile([P, K], U32, name="dpa_codes%d" % g, align_bytes=64) for g in range(GROUPS)]
        dpa_scales = [keep.tile([P, K], U8, name="dpa_scales%d" % g, align_bytes=64) for g in range(GROUPS)]
        z_il = [keep.tile([P, W, T], BF16, name="z_il%d" % g, align_bytes=64) for g in range(GROUPS)]
        z_codes = [keep.tile([P, W], U32, name="z_codes%d" % g, align_bytes=64) for g in range(GROUPS)]
        z_scales = [keep.tile([P, W], U8, name="z_scales%d" % g, align_bytes=64) for g in range(GROUPS)]

        cw_v = C_w.rearrange("(p j) k -> p j k", j=T)
        g_v = grad_out.rearrange("(g p j) o -> g p j o", g=GROUPS, j=T)
        x2_v = x2.rearrange("(g p j) k -> g p j k", g=GROUPS, j=T)
        z_v = z.rearrange("(g p j) w -> g p j w", g=GROUPS, j=T)
        t3_v = T3.rearrange("(s i j) w -> i s j w", s=16, i=8, j=8)
        out0_v = out_0.rearrange("(g p t) w -> g t p w", g=GROUPS, t=T)
        out1_v = out_1.rearrange("(s i j) w -> i s j w", s=16, i=8, j=8)

        psum = {}
        taken = []
        in_turn = []

        def next_bank(width=N, dtype=F32, bank=None):
            if bank is None:
                bank = len(in_turn) % 8
                in_turn.append(bank)
            taken.append(banks.tile([P, width], dtype, name="bank%d" % bank))
            return taken[-1][:]

        sbuf = {}

        def copy(engine, out, in_):
            if engine == "V":
                nc.vector.tensor_copy(out=out, in_=in_)
            elif engine == "S":
                nc.scalar.copy(out=out, in_=in_)
            else:
                nc.gpsimd.tensor_scalar(out=out, in0=in_, scalar1=1.0, scalar2=0.0, op0=MULT, op1=ADD)

        def quantize(codes, scales, values, fmt):
            nc.vector.quantize_mx(out=codes.bitcast(fmt), scales=scales, in_=values)

        def t3_windows(h, l):
            by_u = t3_raw[h][:, L_STEP * l : L_STEP * l + 2 * U_STEP]
            return by_u.rearrange("p (u c) -> p u c", u=2)[:, :, 0:WIN1]

        def t3_rows(h):
            return t3_raw[h][:, 0 : T * SPAN].rearrange("p (t c) -> p t c", t=T)

        def load_cw():
            nc.sync.dma_start(out=cw_raw[:], in_=cw_v)

        def load_g_first(b):
            nc.sync.dma_start(out=g_first[b][:], in_=g_v[0, :, 2 * b : 2 * b + 2])

        def load_g_second():
            nc.sync.dma_start(out=g_second[:], in_=g_v[1])

        def load_x2_first(b):
            nc.sync.dma_start(out=x2_first[b][:], in_=x2_v[0, :, 2 * b : 2 * b + 2])

        def load_x2_second():
            nc.sync.dma_start(out=x2_second[:], in_=x2_v[1])

        def load_z(g):
            nc.sync.dma_start(out=z_raw[g][:], in_=z_v[g])

        def load_t3(h):
            for l in range(2):
                for u in range(2):
                    i = 4 * h + 2 * u + l
                    nc.sync.dma_start(out=t3_windows(h, l)[:, u], in_=t3_v[i, :, :, SHIFT * i : SHIFT * i + WIN1])

        def load_mask():
            nc.sync.dma_start(out=mask_few[0:8, :], in_=mask[0:8, 0:WIN1])

        def prepare_mask():
            nc.vector.memset(mask_few[:], 0.0)
            nc.vector.tensor_copy(out=ident_half[:], in_=ident[:])
            nc.vector.tensor_copy(out=picks[:], in_=ident[:, 0:8].unsqueeze(1).to_broadcast([P, 16, 8]))

        def spread_mask():
            psum["mask"] = next_bank(WIN1, BF16)
            nc.tensor.matmul(
                out=psum["mask"], lhsT=picks[:].rearrange("p s j -> p (s j)"), rhs=mask_few[:], start=True, stop=True
            )

        def mask_copy():
            nc.scalar.copy(out=mask_row[:], in_=psum["mask"])

        def store_0(g, t):
            nc.sync.dma_start(out=out0_v[g, t], in_=sbuf["res0", g, t][:])

        def store_1(i):
            cols = slice(SHIFT * i, SHIFT * i + WIN1)
            nc.sync.dma_start(out=out1_v[i, :, :, cols], in_=row1[:, i])

        def zero_1(i):
            for first, last in ((0, SHIFT * i), (SHIFT * i + WIN1, W)):
                if last > first:
                    source = zero_row[32:96, 0 : last - first].unsqueeze(1).to_broadcast([64, 2, last - first])
                    nc.sync.dma_start(out=out1_v[i, :, :, first:last], in_=source)

        def g_transpose(g, b):
            ps = next_bank().rearrange("p (a u m) -> p a u m", a=2, u=2)
            for a in range(2):
                words = g_raw[g][b][:, a, :].bitcast(F32)
                for u in range(2):
                    nc.tensor.transpose(ps[:, a, u, :], words[:, u : O // 2 : 2], ident[:])
            psum["g", g, b] = ps

        def g_copy(g, b, engine="S"):
            il = stage.tile([P, 2, P, 2], F32, name="words_il", align_bytes=64, bufs=2)
            copy(engine, il[:], psum["g", g, b][:].rearrange("p a u m -> p a m u"))
            sbuf["g", g, b] = il

        def g_quantize(g, b):
            quantize(
                g_codes[g][:, 2 * b : 2 * b + 2].rearrange("p t m -> p (t m)"),
                g_scales[g][:, 2 * b : 2 * b + 2].rearrange("p t m -> p (t m)"),
                sbuf["g", g, b][:].rearrange("p t m u -> p (t m u)").bitcast(BF16),
                E5M2,
            )

        def cw_copy(h, u, s0, s1, engine):
            src = cw_raw[:].rearrange("p j (s h u r) -> p h u s r j", s=16, h=2, u=2, r=16)[:, h, u, s0:s1]
            dst = cw_il[:, h].rearrange("p (u s r) j -> p u s r j", u=2, s=16, r=16)[:, u, s0:s1]
            if engine == "V":
                nc.vector.tensor_scalar(out=dst, in0=src, scalar1=2.0, scalar2=None, op0=MULT)
            else:
                nc.scalar.activation(out=dst, in_=src, func=COPY, scale=2.0)

        def cw_quantize(h):
            quantize(cw_codes[:, h, :], cw_scales[:, h, :], cw_il[:, h].rearrange("p n j -> p (n j)"), E4M3)

        def dx3(g, t, h):
            ps = next_bank()
            nc.tensor.matmul_mx(
                out=ps[:],
                lhsT=g_codes[g][:, t, :].bitcast(E5M2),
                lhsT_scale=g_scales[g][:, t, :],
                rhs=cw_codes[:, h, :].bitcast(E4M3),
                rhs_scale=cw_scales[:, h, :],
                start=True,
                stop=True,
            )
            psum["dx", g, t, h] = ps

        def dp3(g, t, h):
            x2_p = x2_raw[g][t // 2][:, t % 2, :].rearrange("p (s h u l j) -> p h s l j u", s=16, h=2, u=2, l=2)
            nc.vector.tensor_tensor(
                out=dp[g][:, t, N * h : N * (h + 1)].rearrange("p (l s j u) -> p s l j u", l=2, s=16, u=2),
                in0=psum["dx", g, t, h][:].rearrange("p (u s l j) -> p s l j u", u=2, s=16, l=2),
                in1=x2_p[:, h],
                op=MULT,
            )

        def dpt_transpose(g, t):
            ps = next_bank().rearrange("p (a u m) -> p a u m", a=2, u=2)
            words = dp_flat[g][:, K * t : K * (t + 1)].bitcast(F32)
            for h in range(2):
                for u in range(2):
                    n = P * (2 * h + u)
                    nc.tensor.transpose(ps[:, h, u, :], words[:, n : n + P], ident[:])
            psum["dpt", g, t] = ps

        def dpt_copy(g, t, engine="S"):
            if t % 2 == 0:
                name = "held" if (g, t) == (0, HOLD) else "dpt_il%d%d" % (g, t)
                sbuf["dpt", g, t // 2] = keep.tile([P, 2, 2, P, 2], F32, name=name, align_bytes=64)
            copy(engine, sbuf["dpt", g, t // 2][:, t % 2], psum["dpt", g, t][:].rearrange("p h u m -> p h m u"))

        def dpt_quantize(g, t0, t1):
            quantize(
                dpt_codes[g][:, t0:t1].rearrange("p t h m -> p (t h m)"),
                dpt_scales[g][:, t0:t1].rearrange("p t h m -> p (t h m)"),
                sbuf["dpt", g, t0 // 2][:, t0 % 2 : t0 % 2 + t1 - t0].rearrange("p t h m u -> p (t h m u)").bitcast(BF16),
                E5M2,
            )

        def dpa_piece(g, c):
            if (g, c // 2) not in sbuf:
                name = "held" if (g, c // 2) == (0, 1) else "dpa_il%d%d" % (g, c // 2)
                sbuf[g, c // 2] = keep.tile([P, N, T], BF16, name=name, align_bytes=64)
            return sbuf[g, c // 2][:, 256 * (c % 2) : 256 * (c % 2 + 1), :]

        def dpa_copy(g, c, engine, m0=0, m1=P):
            src = dp[g][:, :, 256 * c : 256 * (c + 1)]
            dst = dpa_piece(g, c)
            if engine == "G":
                copy(
                    engine,
                    dst.rearrange("p (u m) t -> p u m t", u=2)[:, :, m0:m1],
                    src.rearrange("p t (m u) -> p u m t", u=2)[:, :, m0:m1],
                )
            else:
                copy(
                    engine,
                    dst.rearrange("p (u m i) t -> p u m t i", u=2, i=4)[:, :, m0 // 4 : m1 // 4],
                    src.rearrange("p t (m i u) -> p u m t i", u=2, i=4)[:, :, m0 // 4 : m1 // 4],
                )

        def dpa_quantize(g, c0, c1):
            n = slice(256 * c0, 256 * c1)
            values = dpa_piece(g, c0) if c1 == c0 + 1 else sbuf[g, c0 // 2][:]
            quantize(dpa_codes[g][:, n], dpa_scales[g][:, n], values.rearrange("p n t -> p (n t)"), E5M2)

        def interleave(engine, il, rows):
            if engine == "G":
                copy(engine, il, rows.rearrange("p t c -> p c t"))
            else:
                copy(engine, il.rearrange("p (c i) t -> p c t i", i=4), rows.rearrange("p t (c i) -> p c t i", i=4))

        def dpa_weave(g, c, bank):
            ps = next_bank(2 * N, BF16, bank)
            out = ps.rearrange("p (u a m t) -> p a t m u", u=2, a=2, t=T)
            rows = dp[g][:, :, 256 * c : 256 * (c + 1)].rearrange("p t (a e) -> p a t e", a=2)
            for a in range(2):
                nc.tensor.matmul(out=out[:, a], lhsT=ident_half[:], rhs=rows[:, a], start=True, stop=True)
            psum["dpa", g, c] = ps

        def dpa_fetch(g, c):
            out = dpa_piece(g, c).rearrange("p n t -> p (n t)")
            nc.scalar.copy(out=out.bitcast(F32), in_=psum["dpa", g, c].bitcast(F32))

        def m_multiply(h):
            for l in range(2):
                nc.vector.tensor_tensor(
                    out=t3_windows(h, l),
                    in0=t3_windows(h, l),
                    in1=psum["mask"].unsqueeze(1).to_broadcast([P, 2, WIN1]),
                    op=MULT,
                )

        def m_copy(h, a, b, engine):
            interleave(engine, m_il[h][:, a:b, :], t3_rows(h)[:, :, a:b])

        def m_quantize():
            for n in (slice(0, W), slice(W, 2 * SPAN)):
                quantize(m_codes[:, n], m_scales[:, n], m_both[:, n].rearrange("p n t -> p (n t)"), E4M3)

        def z_copy(g, a, b, engine):
            interleave(engine, z_il[g][:, a:b, :], z_raw[g][:, :, a:b])

        def z_quantize(g, a, b):
            n = slice(a, b)
            quantize(z_codes[g][:, n], z_scales[g][:, n], z_il[g][:, n, :].rearrange("p n t -> p (n t)"), E4M3)

        def product_0(g, t, w, bank):
            ps = next_bank(N, F32, bank)
            overlap = (N - P) * (1 - w)
            for h, first, width, out in (
                (w, (SPAN + P) * w, N, ps),
                (1 - w, SPAN * (1 - w) + N * w, P, ps[:, overlap : overlap + P]),
            ):
                nc.tensor.matmul_mx(
                    out=out,
                    lhsT=dpt_codes[g][:, t, h, :].bitcast(E5M2),
                    lhsT_scale=dpt_scales[g][:, t, h, :],
                    rhs=m_codes[:, first : first + width].bitcast(E4M3),
                    rhs_scale=m_scales[:, first : first + width],
                    start=(h == w),
                    stop=(h != w),
                )
            psum["o0", g, t, w] = ps

        def result_0(g, t, w, engine="S"):
            if ("res0", g, t) not in sbuf:
                sbuf["res0", g, t] = stage0.tile([P, W], F32, name="res0")
            copy(engine, sbuf["res0", g, t][:, N * w : N * (w + 1)], psum["o0", g, t, w][:])

        def window(i):
            return SHIFT * i // 64 * 64

        def pass_1(i, g, first=0, bank=None):
            base = window(i)
            col = N * (i // 4) + 256 * (i % 2) + P * (i // 2 % 2)
            if g == first:
                psum["o1", i] = next_bank(COVER, F32, bank)
            for a, b in ((0, 256), (256, COVER)):
                nc.tensor.matmul_mx(
                    out=psum["o1", i][:, a:b],
                    lhsT=dpa_codes[g][:, col : col + P].bitcast(E5M2),
                    lhsT_scale=dpa_scales[g][:, col : col + P],
                    rhs=z_codes[g][:, base + a : base + b].bitcast(E4M3),
                    rhs_scale=z_scales[g][:, base + a : base + b],
                    start=(g == first and a == 0),
                    stop=(g != first and a > 0),
                )

        def product_1(i, bank):
            for g in range(GROUPS):
                pass_1(i, g, 0, bank)

        def result_1(i):
            first = SHIFT * i - window(i)
            nc.vector.tensor_tensor(
                out=row1[:, i],
                in0=psum["o1", i][:, first : first + WIN1],
                in1=mask_row[:],
                op=MULT,
            )

        def fill_zeros():
            for h in range(2):
                rows = t3_rows(h)
                for t in range(T):
                    first = SHIFT * (2 * (t % 2) + t // 2)
                    if first > 0:
                        nc.vector.memset(rows[:, t, 0:first], 0.0)
                    if first + WIN1 < SPAN:
                        nc.vector.memset(rows[:, t, first + WIN1 : SPAN], 0.0)
            for part in (32, 64):
                nc.gpsimd.memset(zero_row[part : part + 32, :].bitcast(U32), 0)

        with tc.manual_schedule():

            def dx_dp(g, t, h):
                dx3(g, t, h)
                dp3(g, t, h)

            def turn(g, t):
                dpt_transpose(g, t)
                dpt_copy(g, t)

            def g_turn(g, b):
                g_transpose(g, b)
                g_copy(g, b)

            def products_0(g, t, pair=(None, None)):
                for w in range(2):
                    product_0(g, t, w, pair[w])

            def results_0(g, t, engines="SS"):
                for w in range(2):
                    result_0(g, t, w, engines[w])
                store_0(g, t)

            def finish_1(i):
                result_1(i)
                store_1(i)

            make_identity(nc, ident[:])
            prepare_mask()
            fill_zeros()
            load_g_first(0)
            load_cw()
            load_mask()
            load_g_first(1)
            load_t3(0)
            load_x2_first(0)
            load_t3(1)
            load_x2_first(1)
            load_g_second()
            load_z(0)
            load_x2_second()
            load_z(1)
            for i in FILL[:6]:
                zero_1(i)

            cw_copy(0, 0, 0, 16, "V")
            cw_copy(0, 1, 0, 5, "V")
            cw_copy(0, 1, 5, 16, "S")
            g_turn(0, 0)
            spread_mask()
            cw_copy(1, 0, 0, 12, "V")
            cw_quantize(0)
            g_quantize(0, 0)
            mask_copy()
            cw_copy(1, 0, 12, 16, "S")
            g_turn(0, 1)
            cw_copy(1, 1, 0, 16, "S")
            m_multiply(0)
            m_copy(0, 0, 192, "G")
            m_copy(0, 192, SPAN, "S")
            g_quantize(0, 1)
            dx_dp(0, 0, 0)
            dx_dp(0, 1, 0)
            cw_quantize(1)
            m_multiply(1)
            m_copy(1, 0, 208, "G")
            m_copy(1, 208, SPAN, "S")
            dx_dp(0, 2, 0)
            dx_dp(0, 3, 0)
            dpa_copy(0, 0, "G")
            for t in range(T):
                dx3(0, t, 1)
            g_turn(1, 0)
            g_turn(1, 1)
            for t in range(T):
                dp3(0, t, 1)
            for t in range(T):
                turn(0, t)

            g_quantize(1, 0)
            m_quantize()
            g_quantize(1, 1)
            dpt_quantize(0, 0, 1)
            dpt_quantize(0, 1, 2)
            dpt_quantize(0, 2, 4)
            dpa_copy(0, 2, "G")
            z_copy(0, 768, 1024, "G")
            dpa_copy(0, 1, "G", 0, 48)
            for t in range(2):
                for h in range(2):
                    dx3(1, t, h)
            z_copy(0, 0, 512, "S")
            products_0(0, 0)
            results_0(0, 0)
            for t in range(2):
                for h in range(2):
                    dp3(1, t, h)
            for h in range(2):
                dx3(1, 2, h)
            products_0(0, 1)
            results_0(0, 1)
            z_copy(0, 512, 768, "S")
            zero_1(FILL[6])
            for h in range(2):
                dx3(1, 3, h)
            turn(1, 0)
            turn(1, 1)
            for t in range(2, 4):
                for h in range(2):
                    dp3(1, t, h)
            products_0(0, 2)
            results_0(0, 2)
            zero_1(FILL[7])
            turn(1, 2)
            turn(1, 3)
            dpa_copy(0, 1, "V", 48, P)
            z_copy(1, 0, 512, "V")
            dpt_quantize(1, 0, 2)
            z_quantize(0, 0, 512)
            for c in range(2):
                dpa_copy(1, c, "V")
            dpt_quantize(1, 2, 4)
            products_0(0, 3)
            results_0(0, 3)
            z_quantize(1, 0, 512)
            dpa_quantize(0, 0, 2)
            dpa_quantize(1, 0, 2)
            z_copy(1, 512, 1024, "V")
            dpa_weave(1, 2, 5)
            products_0(1, 0, (6, 7))
            results_0(1, 0)
            products_0(1, 1, (0, 1))
            results_0(1, 1)
            dpa_weave(0, 3, 2)
            products_0(1, 2, (3, 4))
            results_0(1, 2)
            products_0(1, 3, (6, 7))
            results_0(1, 3)
            product_1(0, 0)
            product_1(1, 1)
            dpa_weave(1, 3, 3)
            dpa_fetch(1, 2)
            dpa_fetch(0, 3)
            dpa_fetch(1, 3)
            z_quantize(0, 512, 1024)
            z_quantize(1, 512, 1024)
            product_1(2, 4)
            product_1(3, 6)
            finish_1(0)
            finish_1(1)
            dpa_quantize(0, 2, 3)
            dpa_quantize(1, 2, 3)
            product_1(4, 7)
            product_1(6, 0)
            finish_1(2)
            dpa_quantize(0, 3, 4)
            dpa_quantize(1, 3, 4)
            product_1(5, 1)
            product_1(7, 5)
            for i in (3, 4, 6, 5, 7):
                finish_1(i)
